import numpy as np
import ml_dtypes

BF16 = ml_dtypes.bfloat16


def bf(x):
    return np.asarray(x, np.float32).astype(BF16)


def f32(x):
    return np.asarray(x, np.float32)


def f64(x):
    return np.asarray(x).astype(np.float64)


def striped(idx):
    return np.tile(idx.reshape(-1, 16).T, (8, 1))


C, S, K, HEADS, DH, M, N, RUN, RUNS = 128, 512, 8, 8, 16, 256, 4096, 256, 16
TERMS = 150


def erf(a):
    a = np.asarray(a, np.float64)
    z = np.clip(a, -6.0, 6.0)
    term = z.copy()
    total = z.copy()
    for n in range(1, TERMS):
        term = term * 2.0 * z * z / (2 * n + 1)
        total = total + term
    val = 2.0 / np.sqrt(np.pi) * np.exp(-z * z) * total
    return np.where(np.abs(a) > 6.0, np.sign(a), val)


def gelu(v):
    return 0.5 * v * (1.0 + erf(v / np.sqrt(2.0)))


def setup_inputs():
    x = bf(np.random.standard_normal((C, S)))
    wkv = bf(1.5 * np.random.standard_normal((C, M)) / np.sqrt(C))
    wqr = bf(1.5 * np.random.standard_normal((C, M)) / np.sqrt(C))
    bqr = f32(0.1 * np.random.standard_normal((M, 1)))
    same_head = bf(np.kron(np.eye(HEADS), np.ones((DH, DH))))
    idx = np.concatenate([np.random.permutation(S)[:RUN] for _ in range(RUNS)])
    return {"x": x, "wkv": wkv, "wqr": wqr, "bqr": bqr, "same_head": same_head, "offs": striped(idx)}


def reference(x, wkv, wqr, bqr, same_head, offs):
    idx = offs[:16].T.reshape(-1)
    h = gelu(f64(x))
    kv = f64(wkv).T @ h[:, idx]
    qr = f64(wqr).T @ h + f64(bqr)
    key, val = kv[:C], kv[C:]
    q, res = qr[:C], qr[C:]
    prod = np.repeat(q, K, axis=1) * key
    score = f64(same_head).T @ prod / np.sqrt(DH)
    e = np.exp(score).reshape(C, S, K)
    att = (e * val.reshape(C, S, K)).sum(axis=2) / e.sum(axis=2)
    return gelu(att + res)

@@ -1,0 +1,192 @@
+import math
+
+import concourse.mybir as mybir
+from concourse.masks import make_identity
+
+BF16, F32, U16 = mybir.dt.bfloat16, mybir.dt.float32, mybir.dt.uint16
+ALU = mybir.AluOpType
+ACT = mybir.ActivationFunctionType
+X_AXIS = mybir.AxisListType.X
+
+C = 128
+S = 512
+K = 8
+DH = 16
+N = S * K
+PIECE = 512
+NODES = PIECE // K
+PIECES = N // PIECE
+HEADS = C // DH
+BLOCK = 128
+BLOCKS = S // BLOCK
+PAIR = 2
+PER_BLOCK = BLOCK // NODES
+PER_BANK = 4
+EARLY = 1
+HELPED = (0, 1)
+UNSUMMED = (2, PER_BANK)
+
+FLOPS = 2 * C * (2 * C) * N + 2 * C * (2 * C) * S + 2 * C * C * N
+
+
+def tile_attnno_kernel(tc, x, wkv, wqr, bqr, same_head, offs, out):
+    nc = tc.nc
+    with (
+        tc.tile_pool(name="held", bufs=1) as held,
+        tc.tile_pool(name="work", bufs=2) as work,
+        tc.tile_pool(name="terms", bufs=BLOCKS) as terms,
+        tc.psum_pool(name="banks", bufs=3) as banks,
+        tc.psum_pool(name="turned_banks", bufs=5) as turned_banks,
+    ):
+        offsets = held.tile([C, N // 16], U16, name="offsets")
+        x_sb = held.tile([C, S], BF16, name="x_sb")
+        wkv_sb = held.tile([C, 2 * C], BF16, name="wkv_sb")
+        wqr_sb = held.tile([C, 2 * C], BF16, name="wqr_sb")
+        head_sb = held.tile([C, C], BF16, name="head_sb")
+        biases = held.tile([C, 2], F32, name="biases")
+        bias_q = biases[:, 0:1]
+        bias_res = biases[:, 1:2]
+        nc.sync.dma_start(x_sb[:], x)
+        nc.sync.dma_start(wqr_sb[:], wqr)
+        nc.sync.dma_start(offsets[:], offs)
+        nc.sync.dma_start(wkv_sb[:], wkv)
+        nc.sync.dma_start(biases[:], bqr.rearrange("(a p) o -> p (a o)", p=C))
+        nc.sync.dma_start(head_sb[:], same_head)
+
+        identity = held.tile([BLOCK, BLOCK], F32, name="identity")
+        make_identity(nc, identity[:])
+        head_columns = head_sb[:].rearrange("e (g d) -> e g d", d=DH)[:, :, 0]
+
+        h = held.tile([C, S], BF16, name="h")
+        nc.scalar.activation(h[:], x_sb[:], ACT.Gelu)
+
+        q = held.tile([C, S], F32, name="q")
+        prod = held.tile([C, K, S], BF16, name="prod")
+        val = held.tile([C, BLOCKS, K, BLOCK], F32, name="val")
+        result = held.tile([C, S], F32, name="result")
+
+        def nodes_of(p):
+            return slice(p * NODES, (p + 1) * NODES)
+
+        def gathered(weight_columns, p, name):
+            bank = banks.tile([C, PIECE], F32, name=name, tag="bank")
+            picked = h[:].indirect(offsets[:, p * (PIECE // 16) : (p + 1) * (PIECE // 16)])
+            nc.tensor.matmul(bank[:], wkv_sb[:, weight_columns], picked, start=True, stop=True)
+            return bank[:].rearrange("c (n t) -> c t n", t=K)
+
+        q_ps = banks.tile([C, S], F32, name="q_ps", tag="bank")
+        nc.tensor.matmul(q_ps[:], wqr_sb[:, 0:C], h[:], start=True, stop=True)
+        for half in (slice(0, S // 2), slice(S // 2, S)):
+            nc.scalar.activation(q[:, half], q_ps[:, half], ACT.Identity, bias=bias_q)
+        exp_table = held.tile([C, 1], F32, name="exp_table")
+        nc.scalar.activation(exp_table[:], q[:, 0:1], ACT.Exp, scale=0.0)
+
+        def values_of_piece(p):
+            value = gathered(slice(C, 2 * C), p, "val_ps")
+            b, k = divmod(p, PER_BLOCK)
+            step = PER_BANK if p == PIECES - 1 else K
+            for first in range(0, K, step):
+                part = slice(first, first + step)
+                nc.scalar.copy(val[:, b, part, k * NODES : (k + 1) * NODES], value[:, part, :])
+
+        for p in range(PIECES):
+            key = gathered(slice(0, C), p, "key_ps")
+            nc.vector.tensor_tensor(
+                prod[:, :, nodes_of(p)], key, q[:, nodes_of(p)].unsqueeze(1).to_broadcast([C, K, NODES]), ALU.mult
+            )
+        for p in range(EARLY):
+            values_of_piece(p)
+
+        score_of = []
+        for half in range(BLOCKS // PAIR):
+            score_ps = banks.tile([BLOCK, PAIR, K, HEADS], F32, name="score_ps", tag="bank")
+            for i in range(PAIR):
+                b = half * PAIR + i
+                for t in range(K):
+                    nc.tensor.matmul(
+                        score_ps[:, i, t, :], prod[:, t, b * BLOCK : (b + 1) * BLOCK], head_columns,
+                        start=True, stop=True,
+                    )
+            score_of.append(score_ps[:].rearrange("n i t g -> n i g t"))
+
+        share_of = []
+        for score in score_of:
+            top = work.tile([BLOCK, PAIR, HEADS], F32, name="top")
+            nc.vector.tensor_reduce(top[:], score, X_AXIS, ALU.max)
+            share = work.tile([BLOCK, PAIR, HEADS, K], F32, name="share")
+            nc.vector.tensor_tensor(
+                share[:], score, top[:].unsqueeze(3).to_broadcast([BLOCK, PAIR, HEADS, K]), ALU.subtract
+            )
+            nc.scalar.activation(share[:], share[:], ACT.Exp, scale=1.0 / math.sqrt(DH))
+            rden = work.tile([BLOCK, PAIR, HEADS], F32, name="rden")
+            nc.vector.tensor_reduce(rden[:], share[:], X_AXIS, ALU.add)
+            nc.vector.reciprocal(rden[:], rden[:])
+            nc.vector.tensor_tensor(
+                share[:], share[:], rden[:].unsqueeze(3).to_broadcast([BLOCK, PAIR, HEADS, K]), ALU.mult
+            )
+            share_of.append(share)
+
+        def weighted_values(b, first, t_inside):
+            turned_ps = turned_banks.tile([BLOCK, PER_BANK, C], F32, name="turned_ps")
+            for t in range(PER_BANK):
+                nc.tensor.transpose(turned_ps[:, t, :], val[:, b, first + t, :], identity[:])
+            turned = turned_ps[:].rearrange("n t (g d) -> n t g d", d=DH)
+            share = share_of[b // PAIR][:, b % PAIR, :, first : first + PER_BANK]
+            if t_inside:
+                weighted = terms.tile([BLOCK, C, PER_BANK], F32, name="weighted", tag="weighted%d" % first)
+                nc.vector.tensor_tensor(
+                    weighted[:].rearrange("n (g d) t -> n g d t", d=DH),
+                    turned.rearrange("n t g d -> n g d t"),
+                    share.unsqueeze(2).to_broadcast([BLOCK, HEADS, DH, PER_BANK]),
+                    ALU.mult,
+                )
+            else:
+                weighted = terms.tile([BLOCK, PER_BANK, C], F32, name="weighted", tag="weighted%d" % first)
+                nc.vector.tensor_tensor(
+                    weighted[:].rearrange("n t (g d) -> n t g d", d=DH),
+                    turned,
+                    share.rearrange("n g t -> n t g").unsqueeze(3).to_broadcast([BLOCK, PER_BANK, HEADS, DH]),
+                    ALU.mult,
+                )
+            return weighted
+
+        def terms_of_block(b):
+            if b in HELPED:
+                products = [weighted_values(b, first, False) for first in range(0, K, PER_BANK)]
+                four = terms.tile([BLOCK, PER_BANK, C], F32, name="four")
+                nc.gpsimd.tensor_tensor(four[:], products[0][:], products[1][:], ALU.add)
+                two = terms.tile([BLOCK, 2, C], F32, name="two")
+                nc.gpsimd.tensor_tensor(two[:], four[:, 0:2, :], four[:, 2:4, :], ALU.add)
+                return [two[:, 0, :], two[:, 1, :]]
+            left = []
+            for first in range(0, K, PER_BANK):
+                if (b, first) == UNSUMMED:
+                    weighted = weighted_values(b, first, False)
+                    left += [weighted[:, t, :] for t in range(PER_BANK)]
+                else:
+                    weighted = weighted_values(b, first, True)
+                    part = terms.tile([BLOCK, C], F32, name="part", tag="part%d" % first)
+                    nc.vector.tensor_reduce(part[:], weighted[:], X_AXIS, ALU.add)
+                    left.append(part[:])
+            return left
+
+        def mean_of_block(b, last_terms):
+            columns = slice(b * BLOCK, (b + 1) * BLOCK)
+            for i, term in enumerate(last_terms):
+                nc.tensor.matmul(out_ps[:, columns], term, identity[:], start=(i == 0), stop=False)
+            nc.tensor.matmul(out_ps[:, columns], wqr_sb[:, C : 2 * C], h[:, columns], start=False, stop=True)
+
+        terms_of = []
+        for b in range(BLOCKS + 1):
+            if b < BLOCKS:
+                for p in range(max(EARLY, b * PER_BLOCK), (b + 1) * PER_BLOCK):
+                    values_of_piece(p)
+            if b > 0:
+                terms_of.append(terms_of_block(b - 1))
+        out_ps = banks.tile([C, S], F32, name="out_ps", tag="bank")
+        for b in (0, 2, 1, 3):
+            mean_of_block(b, terms_of[b])
+
+        for columns in (slice(0, S - BLOCK), slice(S - BLOCK, S)):
+            nc.scalar.activation(result[:, columns], out_ps[:, columns], ACT.Gelu, bias=bias_res)
+            nc.sync.dma_start(out[:, columns], result[:, columns])

@@ -173,7 +173,7 @@ def tile_attnno_kernel(tc, x, wkv, wqr, bqr, same_head, offs, out):
         def mean_of_block(b, last_terms):
             columns = slice(b * BLOCK, (b + 1) * BLOCK)
             for i, term in enumerate(last_terms):
-                nc.tensor.matmul(out_ps[:, columns], term, identity[:], start=(i == 0), stop=False)
+                nc.tensor.matmul(out_ps[:, columns], term, identity[:], start=(i == 0), stop=False, is_transpose=True)
             nc.tensor.matmul(out_ps[:, columns], wqr_sb[:, C : 2 * C], h[:, columns], start=False, stop=True)
 
         terms_of = []

@@ -151,24 +151,8 @@ def tile_attnno_kernel(tc, x, wkv, wqr, bqr, same_head, offs, out):
             return weighted
 
         def terms_of_block(b):
-            if b in HELPED:
-                products = [weighted_values(b, first, False) for first in range(0, K, PER_BANK)]
-                four = terms.tile([BLOCK, PER_BANK, C], F32, name="four")
-                nc.gpsimd.tensor_tensor(four[:], products[0][:], products[1][:], ALU.add)
-                two = terms.tile([BLOCK, 2, C], F32, name="two")
-                nc.gpsimd.tensor_tensor(two[:], four[:, 0:2, :], four[:, 2:4, :], ALU.add)
-                return [two[:, 0, :], two[:, 1, :]]
-            left = []
-            for first in range(0, K, PER_BANK):
-                if (b, first) == UNSUMMED:
-                    weighted = weighted_values(b, first, False)
-                    left += [weighted[:, t, :] for t in range(PER_BANK)]
-                else:
-                    weighted = weighted_values(b, first, True)
-                    part = terms.tile([BLOCK, C], F32, name="part", tag="part%d" % first)
-                    nc.vector.tensor_reduce(part[:], weighted[:], X_AXIS, ALU.add)
-                    left.append(part[:])
-            return left
+            products = [weighted_values(b, first, False) for first in range(0, K, PER_BANK)]
+            return [weighted[:, t, :] for weighted in products for t in range(PER_BANK)]
 
         def mean_of_block(b, last_terms):
             columns = slice(b * BLOCK, (b + 1) * BLOCK)
@@ -184,7 +168,7 @@ def tile_attnno_kernel(tc, x, wkv, wqr, bqr, same_head, offs, out):
             if b > 0:
                 terms_of.append(terms_of_block(b - 1))
         out_ps = banks.tile([C, S], F32, name="out_ps", tag="bank")
-        for b in (0, 2, 1, 3):
+        for b in range(BLOCKS):
             mean_of_block(b, terms_of[b])
 
         for columns in (slice(0, S - BLOCK), slice(S - BLOCK, S)):

@@ -22,9 +22,7 @@ BLOCKS = S // BLOCK
 PAIR = 2
 PER_BLOCK = BLOCK // NODES
 PER_BANK = 4
-EARLY = 1
-HELPED = (0, 1)
-UNSUMMED = (2, PER_BANK)
+HALVES = BLOCKS * K // PER_BANK
 
 FLOPS = 2 * C * (2 * C) * N + 2 * C * (2 * C) * S + 2 * C * C * N
 
@@ -33,10 +31,7 @@ def tile_attnno_kernel(tc, x, wkv, wqr, bqr, same_head, offs, out):
     nc = tc.nc
     with (
         tc.tile_pool(name="held", bufs=1) as held,
-        tc.tile_pool(name="work", bufs=2) as work,
-        tc.tile_pool(name="terms", bufs=BLOCKS) as terms,
-        tc.psum_pool(name="banks", bufs=3) as banks,
-        tc.psum_pool(name="turned_banks", bufs=5) as turned_banks,
+        tc.psum_pool(name="psum", bufs=1) as psum,
     ):
         offsets = held.tile([C, N // 16], U16, name="offsets")
         x_sb = held.tile([C, S], BF16, name="x_sb")
@@ -57,32 +52,39 @@ def tile_attnno_kernel(tc, x, wkv, wqr, bqr, same_head, offs, out):
         make_identity(nc, identity[:])
         head_columns = head_sb[:].rearrange("e (g d) -> e g d", d=DH)[:, :, 0]
 
+        banks = [psum.tile([C, PIECE], F32, name="bank%d" % i) for i in range(8)]
+        key_banks = banks[0:4]
+        query_bank, first_value_bank = banks[4], banks[5]
+        score_banks = [banks[0], banks[6]]
+        out_banks = [banks[1], banks[2]]
+        value_banks = [banks[3], banks[0], banks[6]]
+        turned_banks = [banks[4], banks[7], banks[5]]
+
         h = held.tile([C, S], BF16, name="h")
         nc.scalar.activation(h[:], x_sb[:], ACT.Gelu)
 
         q = held.tile([C, S], F32, name="q")
         prod = held.tile([C, K, S], BF16, name="prod")
         val = held.tile([C, BLOCKS, K, BLOCK], F32, name="val")
+        weighted = held.tile([BLOCK, HALVES, PER_BANK, C], F32, name="weighted")
         result = held.tile([C, S], F32, name="result")
 
         def nodes_of(p):
             return slice(p * NODES, (p + 1) * NODES)
 
-        def gathered(weight_columns, p, name):
-            bank = banks.tile([C, PIECE], F32, name=name, tag="bank")
+        def gathered(bank, weight_columns, p):
             picked = h[:].indirect(offsets[:, p * (PIECE // 16) : (p + 1) * (PIECE // 16)])
             nc.tensor.matmul(bank[:], wkv_sb[:, weight_columns], picked, start=True, stop=True)
             return bank[:].rearrange("c (n t) -> c t n", t=K)
 
-        q_ps = banks.tile([C, S], F32, name="q_ps", tag="bank")
-        nc.tensor.matmul(q_ps[:], wqr_sb[:, 0:C], h[:], start=True, stop=True)
+        nc.tensor.matmul(query_bank[:], wqr_sb[:, 0:C], h[:], start=True, stop=True)
         for half in (slice(0, S // 2), slice(S // 2, S)):
-            nc.scalar.activation(q[:, half], q_ps[:, half], ACT.Identity, bias=bias_q)
+            nc.scalar.activation(q[:, half], query_bank[:, half], ACT.Identity, bias=bias_q)
         exp_table = held.tile([C, 1], F32, name="exp_table")
         nc.scalar.activation(exp_table[:], q[:, 0:1], ACT.Exp, scale=0.0)
 
-        def values_of_piece(p):
-            value = gathered(slice(C, 2 * C), p, "val_ps")
+        def values_of_piece(p, bank):
+            value = gathered(bank, slice(C, 2 * C), p)
             b, k = divmod(p, PER_BLOCK)
             step = PER_BANK if p == PIECES - 1 else K
             for first in range(0, K, step):
@@ -90,16 +92,14 @@ def tile_attnno_kernel(tc, x, wkv, wqr, bqr, same_head, offs, out):
                 nc.scalar.copy(val[:, b, part, k * NODES : (k + 1) * NODES], value[:, part, :])
 
         for p in range(PIECES):
-            key = gathered(slice(0, C), p, "key_ps")
+            key = gathered(key_banks[p % len(key_banks)], slice(0, C), p)
             nc.vector.tensor_tensor(
                 prod[:, :, nodes_of(p)], key, q[:, nodes_of(p)].unsqueeze(1).to_broadcast([C, K, NODES]), ALU.mult
             )
-        for p in range(EARLY):
-            values_of_piece(p)
+        values_of_piece(0, first_value_bank)
 
-        score_of = []
-        for half in range(BLOCKS // PAIR):
-            score_ps = banks.tile([BLOCK, PAIR, K, HEADS], F32, name="score_ps", tag="bank")
+        def scores_of_pair(half):
+            score_ps = score_banks[half][:, 0 : PAIR * K * HEADS].rearrange("n (i t g) -> n i t g", t=K, g=HEADS)
             for i in range(PAIR):
                 b = half * PAIR + i
                 for t in range(K):
@@ -107,70 +107,68 @@ def tile_attnno_kernel(tc, x, wkv, wqr, bqr, same_head, offs, out):
                         score_ps[:, i, t, :], prod[:, t, b * BLOCK : (b + 1) * BLOCK], head_columns,
                         start=True, stop=True,
                     )
-            score_of.append(score_ps[:].rearrange("n i t g -> n i g t"))
+            return score_ps.rearrange("n i t g -> n i g t")
+
+        out_columns = [slice(0, S - BLOCK), slice(S - BLOCK, S)]
+        score_of = [scores_of_pair(0)]
+        for bank, columns in zip(out_banks, out_columns):
+            nc.tensor.matmul(bank[:, columns], wqr_sb[:, C : 2 * C], h[:, columns], start=True, stop=False)
+        score_of.append(scores_of_pair(1))
 
         share_of = []
-        for score in score_of:
-            top = work.tile([BLOCK, PAIR, HEADS], F32, name="top")
+        for half, score in enumerate(score_of):
+            top = held.tile([BLOCK, PAIR, HEADS], F32, name="top%d" % half)
             nc.vector.tensor_reduce(top[:], score, X_AXIS, ALU.max)
-            share = work.tile([BLOCK, PAIR, HEADS, K], F32, name="share")
+            share = held.tile([BLOCK, PAIR, HEADS, K], F32, name="share%d" % half)
             nc.vector.tensor_tensor(
                 share[:], score, top[:].unsqueeze(3).to_broadcast([BLOCK, PAIR, HEADS, K]), ALU.subtract
             )
             nc.scalar.activation(share[:], share[:], ACT.Exp, scale=1.0 / math.sqrt(DH))
-            rden = work.tile([BLOCK, PAIR, HEADS], F32, name="rden")
+            share_of.append(share)
+
+        def normalise(half):
+            share = share_of[half]
+            rden = held.tile([BLOCK, PAIR, HEADS], F32, name="rden%d" % half)
             nc.vector.tensor_reduce(rden[:], share[:], X_AXIS, ALU.add)
             nc.vector.reciprocal(rden[:], rden[:])
             nc.vector.tensor_tensor(
                 share[:], share[:], rden[:].unsqueeze(3).to_broadcast([BLOCK, PAIR, HEADS, K]), ALU.mult
             )
-            share_of.append(share)
 
-        def weighted_values(b, first, t_inside):
-            turned_ps = turned_banks.tile([BLOCK, PER_BANK, C], F32, name="turned_ps")
+        def turn_and_weigh(u):
+            b, first = u // 2, (u % 2) * PER_BANK
+            turned = turned_banks[u % len(turned_banks)][:].rearrange("n (t c) -> n t c", c=C)
             for t in range(PER_BANK):
-                nc.tensor.transpose(turned_ps[:, t, :], val[:, b, first + t, :], identity[:])
-            turned = turned_ps[:].rearrange("n t (g d) -> n t g d", d=DH)
+                nc.tensor.transpose(turned[:, t, :], val[:, b, first + t, :], identity[:])
             share = share_of[b // PAIR][:, b % PAIR, :, first : first + PER_BANK]
-            if t_inside:
-                weighted = terms.tile([BLOCK, C, PER_BANK], F32, name="weighted", tag="weighted%d" % first)
-                nc.vector.tensor_tensor(
-                    weighted[:].rearrange("n (g d) t -> n g d t", d=DH),
-                    turned.rearrange("n t g d -> n g d t"),
-                    share.unsqueeze(2).to_broadcast([BLOCK, HEADS, DH, PER_BANK]),
-                    ALU.mult,
+            nc.vector.tensor_tensor(
+                weighted[:, u].rearrange("n t (g d) -> n t g d", d=DH),
+                turned.rearrange("n t (g d) -> n t g d", d=DH),
+                share.rearrange("n g t -> n t g").unsqueeze(3).to_broadcast([BLOCK, PER_BANK, HEADS, DH]),
+                ALU.mult,
+            )
+
+        def turn_back(u):
+            b = u // 2
+            bank = out_banks[b // (BLOCKS - 1)]
+            last = u in (HALVES - 3, HALVES - 1)
+            for t in range(PER_BANK):
+                nc.tensor.matmul(
+                    bank[:, b * BLOCK : (b + 1) * BLOCK], weighted[:, u, t, :], identity[:],
+                    start=False, stop=(last and t == PER_BANK - 1), is_transpose=True,
                 )
-            else:
-                weighted = terms.tile([BLOCK, PER_BANK, C], F32, name="weighted", tag="weighted%d" % first)
-                nc.vector.tensor_tensor(
-                    weighted[:].rearrange("n t (g d) -> n t g d", d=DH),
-                    turned,
-                    share.rearrange("n g t -> n t g").unsqueeze(3).to_broadcast([BLOCK, PER_BANK, HEADS, DH]),
-                    ALU.mult,
-                )
-            return weighted
 
-        def terms_of_block(b):
-            products = [weighted_values(b, first, False) for first in range(0, K, PER_BANK)]
-            return [weighted[:, t, :] for weighted in products for t in range(PER_BANK)]
+        normalise(0)
+        for step in range(1, PIECES + 5):
+            if step < PIECES:
+                values_of_piece(step, value_banks[(step - 1) % len(value_banks)])
+            if step == 4:
+                normalise(1)
+            if 0 <= step - 2 < HALVES:
+                turn_and_weigh(step - 2)
+            if 0 <= step - 5 < HALVES:
+                turn_back(step - 5)
 
-        def mean_of_block(b, last_terms):
-            columns = slice(b * BLOCK, (b + 1) * BLOCK)
-            for i, term in enumerate(last_terms):
-                nc.tensor.matmul(out_ps[:, columns], term, identity[:], start=(i == 0), stop=False, is_transpose=True)
-            nc.tensor.matmul(out_ps[:, columns], wqr_sb[:, C : 2 * C], h[:, columns], start=False, stop=True)
-
-        terms_of = []
-        for b in range(BLOCKS + 1):
-            if b < BLOCKS:
-                for p in range(max(EARLY, b * PER_BLOCK), (b + 1) * PER_BLOCK):
-                    values_of_piece(p)
-            if b > 0:
-                terms_of.append(terms_of_block(b - 1))
-        out_ps = banks.tile([C, S], F32, name="out_ps", tag="bank")
-        for b in range(BLOCKS):
-            mean_of_block(b, terms_of[b])
-
-        for columns in (slice(0, S - BLOCK), slice(S - BLOCK, S)):
-            nc.scalar.activation(result[:, columns], out_ps[:, columns], ACT.Gelu, bias=bias_res)
+        for bank, columns in zip(out_banks, out_columns):
+            nc.scalar.activation(result[:, columns], bank[:, columns], ACT.Gelu, bias=bias_res)
             nc.sync.dma_start(out[:, columns], result[:, columns])

@@ -54,14 +54,16 @@ def tile_attnno_kernel(tc, x, wkv, wqr, bqr, same_head, offs, out):
 
         banks = [psum.tile([C, PIECE], F32, name="bank%d" % i) for i in range(8)]
         key_banks = banks[0:4]
-        query_bank, first_value_bank = banks[4], banks[5]
+        query_banks, first_value_bank = [banks[4], banks[7]], banks[5]
         score_banks = [banks[0], banks[6]]
         out_banks = [banks[1], banks[2]]
         value_banks = [banks[3], banks[0], banks[6]]
         turned_banks = [banks[4], banks[7], banks[5]]
 
         h = held.tile([C, S], BF16, name="h")
-        nc.scalar.activation(h[:], x_sb[:], ACT.Gelu)
+        halves = (slice(0, S // 2), slice(S // 2, S))
+        for half in halves:
+            nc.scalar.activation(h[:, half], x_sb[:, half], ACT.Gelu)
 
         q = held.tile([C, S], F32, name="q")
         prod = held.tile([C, K, S], BF16, name="prod")
@@ -77,11 +79,11 @@ def tile_attnno_kernel(tc, x, wkv, wqr, bqr, same_head, offs, out):
             nc.tensor.matmul(bank[:], wkv_sb[:, weight_columns], picked, start=True, stop=True)
             return bank[:].rearrange("c (n t) -> c t n", t=K)
 
-        nc.tensor.matmul(query_bank[:], wqr_sb[:, 0:C], h[:], start=True, stop=True)
-        for half in (slice(0, S // 2), slice(S // 2, S)):
-            nc.scalar.activation(q[:, half], query_bank[:, half], ACT.Identity, bias=bias_q)
+        for bank, half in zip(query_banks, halves):
+            nc.tensor.matmul(bank[:, half], wqr_sb[:, 0:C], h[:, half], start=True, stop=True)
+            nc.scalar.activation(q[:, half], bank[:, half], ACT.Identity, bias=bias_q)
         exp_table = held.tile([C, 1], F32, name="exp_table")
-        nc.scalar.activation(exp_table[:], q[:, 0:1], ACT.Exp, scale=0.0)
+        nc.scalar.activation(exp_table[:], q[:, S - 1 : S], ACT.Exp, scale=0.0)
 
         def values_of_piece(p, bank):
             value = gathered(bank, slice(C, 2 * C), p)

@@ -19,7 +19,6 @@ PIECES = N // PIECE
 HEADS = C // DH
 BLOCK = 128
 BLOCKS = S // BLOCK
-PAIR = 2
 PER_BLOCK = BLOCK // NODES
 PER_BANK = 4
 HALVES = BLOCKS * K // PER_BANK
@@ -53,12 +52,12 @@ def tile_attnno_kernel(tc, x, wkv, wqr, bqr, same_head, offs, out):
         head_columns = head_sb[:].rearrange("e (g d) -> e g d", d=DH)[:, :, 0]
 
         banks = [psum.tile([C, PIECE], F32, name="bank%d" % i) for i in range(8)]
-        key_banks = banks[0:4]
-        query_banks, first_value_bank = [banks[4], banks[7]], banks[5]
-        score_banks = [banks[0], banks[6]]
-        out_banks = [banks[1], banks[2]]
-        value_banks = [banks[3], banks[0], banks[6]]
+        query_banks = [banks[4], banks[7]]
+        key_banks = banks[0:4] + banks[0:4]
+        score_banks = [banks[0], banks[1], banks[6]]
+        value_banks = [banks[5]] + [(banks[3], banks[0], banks[6])[i % 3] for i in range(PIECES - 1)]
         turned_banks = [banks[4], banks[7], banks[5]]
+        out_banks = [banks[2], banks[1]]
 
         h = held.tile([C, S], BF16, name="h")
         halves = (slice(0, S // 2), slice(S // 2, S))
@@ -79,97 +78,114 @@ def tile_attnno_kernel(tc, x, wkv, wqr, bqr, same_head, offs, out):
             nc.tensor.matmul(bank[:], wkv_sb[:, weight_columns], picked, start=True, stop=True)
             return bank[:].rearrange("c (n t) -> c t n", t=K)
 
-        for bank, half in zip(query_banks, halves):
-            nc.tensor.matmul(bank[:, half], wqr_sb[:, 0:C], h[:, half], start=True, stop=True)
-            nc.scalar.activation(q[:, half], bank[:, half], ACT.Identity, bias=bias_q)
-        exp_table = held.tile([C, 1], F32, name="exp_table")
-        nc.scalar.activation(exp_table[:], q[:, S - 1 : S], ACT.Exp, scale=0.0)
+        def keys_of_piece(p):
+            key = gathered(key_banks[p], slice(0, C), p)
+            nc.vector.tensor_tensor(
+                prod[:, :, nodes_of(p)], key, q[:, nodes_of(p)].unsqueeze(1).to_broadcast([C, K, NODES]), ALU.mult
+            )
 
-        def values_of_piece(p, bank):
-            value = gathered(bank, slice(C, 2 * C), p)
+        def values_of_piece(p):
+            value = gathered(value_banks[p], slice(C, 2 * C), p)
             b, k = divmod(p, PER_BLOCK)
             step = PER_BANK if p == PIECES - 1 else K
             for first in range(0, K, step):
                 part = slice(first, first + step)
                 nc.scalar.copy(val[:, b, part, k * NODES : (k + 1) * NODES], value[:, part, :])
 
-        for p in range(PIECES):
-            key = gathered(key_banks[p % len(key_banks)], slice(0, C), p)
-            nc.vector.tensor_tensor(
-                prod[:, :, nodes_of(p)], key, q[:, nodes_of(p)].unsqueeze(1).to_broadcast([C, K, NODES]), ALU.mult
-            )
-        values_of_piece(0, first_value_bank)
+        groups = [range(0, 1), range(1, 2), range(2, BLOCKS)]
 
-        def scores_of_pair(half):
-            score_ps = score_banks[half][:, 0 : PAIR * K * HEADS].rearrange("n (i t g) -> n i t g", t=K, g=HEADS)
-            for i in range(PAIR):
-                b = half * PAIR + i
+        def score_view(group):
+            return score_banks[group][:, 0 : len(groups[group]) * K * HEADS].rearrange(
+                "n (i t g) -> n i t g", t=K, g=HEADS
+            )
+
+        def scores(group):
+            for i, b in enumerate(groups[group]):
                 for t in range(K):
                     nc.tensor.matmul(
-                        score_ps[:, i, t, :], prod[:, t, b * BLOCK : (b + 1) * BLOCK], head_columns,
+                        score_view(group)[:, i, t, :], prod[:, t, b * BLOCK : (b + 1) * BLOCK], head_columns,
                         start=True, stop=True,
                     )
-            return score_ps.rearrange("n i t g -> n i g t")
 
-        out_columns = [slice(0, S - BLOCK), slice(S - BLOCK, S)]
-        score_of = [scores_of_pair(0)]
-        for bank, columns in zip(out_banks, out_columns):
-            nc.tensor.matmul(bank[:, columns], wqr_sb[:, C : 2 * C], h[:, columns], start=True, stop=False)
-        score_of.append(scores_of_pair(1))
+        share = held.tile([BLOCK, BLOCKS, HEADS, K], F32, name="share")
+        top = held.tile([BLOCK, BLOCKS, HEADS], F32, name="top")
+        rden = held.tile([BLOCK, BLOCKS, HEADS], F32, name="rden")
 
-        share_of = []
-        for half, score in enumerate(score_of):
-            top = held.tile([BLOCK, PAIR, HEADS], F32, name="top%d" % half)
-            nc.vector.tensor_reduce(top[:], score, X_AXIS, ALU.max)
-            share = held.tile([BLOCK, PAIR, HEADS, K], F32, name="share%d" % half)
+        def exponentials(group):
+            score = score_view(group).rearrange("n i t g -> n i g t")
+            blocks = slice(groups[group].start, groups[group].stop)
+            shape = [BLOCK, len(groups[group]), HEADS, K]
+            nc.vector.tensor_reduce(top[:, blocks], score, X_AXIS, ALU.max)
             nc.vector.tensor_tensor(
-                share[:], score, top[:].unsqueeze(3).to_broadcast([BLOCK, PAIR, HEADS, K]), ALU.subtract
+                share[:, blocks], score, top[:, blocks].unsqueeze(3).to_broadcast(shape), ALU.subtract
             )
-            nc.scalar.activation(share[:], share[:], ACT.Exp, scale=1.0 / math.sqrt(DH))
-            share_of.append(share)
+            nc.scalar.activation(share[:, blocks], share[:, blocks], ACT.Exp, scale=1.0 / math.sqrt(DH))
 
-        def normalise(half):
-            share = share_of[half]
-            rden = held.tile([BLOCK, PAIR, HEADS], F32, name="rden%d" % half)
-            nc.vector.tensor_reduce(rden[:], share[:], X_AXIS, ALU.add)
-            nc.vector.reciprocal(rden[:], rden[:])
+        def normalise(group):
+            blocks = slice(groups[group].start, groups[group].stop)
+            shape = [BLOCK, len(groups[group]), HEADS, K]
+            nc.vector.tensor_reduce(rden[:, blocks], share[:, blocks], X_AXIS, ALU.add)
+            nc.vector.reciprocal(rden[:, blocks], rden[:, blocks])
             nc.vector.tensor_tensor(
-                share[:], share[:], rden[:].unsqueeze(3).to_broadcast([BLOCK, PAIR, HEADS, K]), ALU.mult
+                share[:, blocks], share[:, blocks], rden[:, blocks].unsqueeze(3).to_broadcast(shape), ALU.mult
             )
 
-        def turn_and_weigh(u):
+        def turned_view(u):
+            return turned_banks[u % len(turned_banks)][:].rearrange("n (t c) -> n t c", c=C)
+
+        def turn(u):
             b, first = u // 2, (u % 2) * PER_BANK
-            turned = turned_banks[u % len(turned_banks)][:].rearrange("n (t c) -> n t c", c=C)
             for t in range(PER_BANK):
-                nc.tensor.transpose(turned[:, t, :], val[:, b, first + t, :], identity[:])
-            share = share_of[b // PAIR][:, b % PAIR, :, first : first + PER_BANK]
+                nc.tensor.transpose(turned_view(u)[:, t, :], val[:, b, first + t, :], identity[:])
+
+        def weigh(u):
+            b, first = u // 2, (u % 2) * PER_BANK
+            part = share[:, b, :, first : first + PER_BANK]
             nc.vector.tensor_tensor(
                 weighted[:, u].rearrange("n t (g d) -> n t g d", d=DH),
-                turned.rearrange("n t (g d) -> n t g d", d=DH),
-                share.rearrange("n g t -> n t g").unsqueeze(3).to_broadcast([BLOCK, PER_BANK, HEADS, DH]),
+                turned_view(u).rearrange("n t (g d) -> n t g d", d=DH),
+                part.rearrange("n g t -> n t g").unsqueeze(3).to_broadcast([BLOCK, PER_BANK, HEADS, DH]),
                 ALU.mult,
             )
+
+        out_columns = [slice(0, S - BLOCK), slice(S - BLOCK, S)]
 
         def turn_back(u):
             b = u // 2
             bank = out_banks[b // (BLOCKS - 1)]
-            last = u in (HALVES - 3, HALVES - 1)
             for t in range(PER_BANK):
                 nc.tensor.matmul(
                     bank[:, b * BLOCK : (b + 1) * BLOCK], weighted[:, u, t, :], identity[:],
-                    start=False, stop=(last and t == PER_BANK - 1), is_transpose=True,
+                    start=(u in (0, HALVES - 2) and t == 0), stop=False, is_transpose=True,
                 )
+            if u in (HALVES - 3, HALVES - 1):
+                columns = out_columns[b // (BLOCKS - 1)]
+                nc.tensor.matmul(bank[:, columns], wqr_sb[:, C : 2 * C], h[:, columns], start=False, stop=True)
 
-        normalise(0)
-        for step in range(1, PIECES + 5):
-            if step < PIECES:
-                values_of_piece(step, value_banks[(step - 1) % len(value_banks)])
-            if step == 4:
-                normalise(1)
-            if 0 <= step - 2 < HALVES:
-                turn_and_weigh(step - 2)
-            if 0 <= step - 5 < HALVES:
-                turn_back(step - 5)
+        for bank, half in zip(query_banks, halves):
+            nc.tensor.matmul(bank[:, half], wqr_sb[:, 0:C], h[:, half], start=True, stop=True)
+            nc.scalar.activation(q[:, half], bank[:, half], ACT.Identity, bias=bias_q)
+        exp_table = held.tile([C, 1], F32, name="exp_table")
+        nc.scalar.activation(exp_table[:], q[:, S - 1 : S], ACT.Exp, scale=0.0)
+
+        for p in range(PIECES):
+            keys_of_piece(p)
+        values_of_piece(0)
+        for stage in (scores, exponentials, normalise):
+            for group in range(len(groups)):
+                stage(group)
+
+        for p in range(1, PIECES - 1):
+            values_of_piece(p)
+            if 2 <= p < PIECES - 2:
+                turn(p - 2)
+                weigh(p - 2)
+        values_of_piece(PIECES - 1)
+        for u in range(PIECES - 4, HALVES):
+            turn(u)
+            weigh(u)
+        for u in range(HALVES):
+            turn_back(u)
 
         for bank, columns in zip(out_banks, out_columns):
             nc.scalar.activation(result[:, columns], bank[:, columns], ACT.Gelu, bias=bias_res)

@@ -156,10 +156,10 @@ def tile_attnno_kernel(tc, x, wkv, wqr, bqr, same_head, offs, out):
             for t in range(PER_BANK):
                 nc.tensor.matmul(
                     bank[:, b * BLOCK : (b + 1) * BLOCK], weighted[:, u, t, :], identity[:],
-                    start=(u in (0, HALVES - 2) and t == 0), stop=False, is_transpose=True,
+                    start=(u == HALVES - 2 and t == 0), stop=(u == HALVES - 3 and t == PER_BANK - 1), is_transpose=True,
                 )
-            if u in (HALVES - 3, HALVES - 1):
-                columns = out_columns[b // (BLOCKS - 1)]
+            if u == HALVES - 1:
+                columns = out_columns[1]
                 nc.tensor.matmul(bank[:, columns], wqr_sb[:, C : 2 * C], h[:, columns], start=False, stop=True)
 
         for bank, half in zip(query_banks, halves):
@@ -171,21 +171,24 @@ def tile_attnno_kernel(tc, x, wkv, wqr, bqr, same_head, offs, out):
         for p in range(PIECES):
             keys_of_piece(p)
         values_of_piece(0)
-        for stage in (scores, exponentials, normalise):
+        scores(0)
+        scores(1)
+        nc.tensor.matmul(
+            out_banks[0][:, out_columns[0]], wqr_sb[:, C : 2 * C], h[:, out_columns[0]], start=True, stop=False
+        )
+        scores(2)
+        for stage in (exponentials, normalise):
             for group in range(len(groups)):
                 stage(group)
 
-        for p in range(1, PIECES - 1):
-            values_of_piece(p)
-            if 2 <= p < PIECES - 2:
-                turn(p - 2)
-                weigh(p - 2)
-        values_of_piece(PIECES - 1)
-        for u in range(PIECES - 4, HALVES):
-            turn(u)
-            weigh(u)
-        for u in range(HALVES):
-            turn_back(u)
+        for step in range(1, PIECES + 5):
+            if step < PIECES:
+                values_of_piece(step)
+            if 0 <= step - 2 < HALVES:
+                turn(step - 2)
+                weigh(step - 2)
+            if 0 <= step - 5 < HALVES:
+                turn_back(step - 5)
 
         for bank, columns in zip(out_banks, out_columns):
             nc.scalar.activation(result[:, columns], bank[:, columns], ACT.Gelu, bias=bias_res)

@@ -53,11 +53,11 @@ def tile_attnno_kernel(tc, x, wkv, wqr, bqr, same_head, offs, out):
 
         banks = [psum.tile([C, PIECE], F32, name="bank%d" % i) for i in range(8)]
         query_banks = [banks[4], banks[7]]
-        key_banks = banks[0:4] + banks[0:4]
-        score_banks = [banks[0], banks[1], banks[6]]
-        value_banks = [banks[5]] + [(banks[3], banks[0], banks[6])[i % 3] for i in range(PIECES - 1)]
-        turned_banks = [banks[4], banks[7], banks[5]]
-        out_banks = [banks[2], banks[1]]
+        key_banks = [banks[i] for i in (0, 1, 2, 3, 5, 6, 4, 7)]
+        score_banks = banks[1:4]
+        value_banks = [banks[0]] + [(banks[7], banks[1], banks[2])[i % 3] for i in range(PIECES - 1)]
+        turned_banks = [banks[0], banks[4], banks[6], banks[3]]
+        out_banks = [banks[5], banks[7]]
 
         h = held.tile([C, S], BF16, name="h")
         halves = (slice(0, S // 2), slice(S // 2, S))
@@ -156,11 +156,12 @@ def tile_attnno_kernel(tc, x, wkv, wqr, bqr, same_head, offs, out):
             for t in range(PER_BANK):
                 nc.tensor.matmul(
                     bank[:, b * BLOCK : (b + 1) * BLOCK], weighted[:, u, t, :], identity[:],
-                    start=(u == HALVES - 2 and t == 0), stop=(u == HALVES - 3 and t == PER_BANK - 1), is_transpose=True,
+                    start=False, stop=(u in (HALVES - 3, HALVES - 1) and t == PER_BANK - 1), is_transpose=True,
                 )
-            if u == HALVES - 1:
-                columns = out_columns[1]
-                nc.tensor.matmul(bank[:, columns], wqr_sb[:, C : 2 * C], h[:, columns], start=False, stop=True)
+
+        def linear_branch(i):
+            columns = out_columns[i]
+            nc.tensor.matmul(out_banks[i][:, columns], wqr_sb[:, C : 2 * C], h[:, columns], start=True, stop=False)
 
         for bank, half in zip(query_banks, halves):
             nc.tensor.matmul(bank[:, half], wqr_sb[:, 0:C], h[:, half], start=True, stop=True)
@@ -173,9 +174,7 @@ def tile_attnno_kernel(tc, x, wkv, wqr, bqr, same_head, offs, out):
         values_of_piece(0)
         scores(0)
         scores(1)
-        nc.tensor.matmul(
-            out_banks[0][:, out_columns[0]], wqr_sb[:, C : 2 * C], h[:, out_columns[0]], start=True, stop=False
-        )
+        linear_branch(0)
         scores(2)
         for stage in (exponentials, normalise):
             for group in range(len(groups)):
@@ -189,6 +188,8 @@ def tile_attnno_kernel(tc, x, wkv, wqr, bqr, same_head, offs, out):
                 weigh(step - 2)
             if 0 <= step - 5 < HALVES:
                 turn_back(step - 5)
+            if step == PIECES - 1:
+                linear_branch(1)
 
         for bank, columns in zip(out_banks, out_columns):
             nc.scalar.activation(result[:, columns], bank[:, columns], ACT.Gelu, bias=bias_res)

@@ -180,16 +180,21 @@ def tile_attnno_kernel(tc, x, wkv, wqr, bqr, same_head, offs, out):
             for group in range(len(groups)):
                 stage(group)
 
-        for step in range(1, PIECES + 5):
-            if step < PIECES:
-                values_of_piece(step)
-            if 0 <= step - 2 < HALVES:
-                turn(step - 2)
-                weigh(step - 2)
-            if 0 <= step - 5 < HALVES:
-                turn_back(step - 5)
-            if step == PIECES - 1:
-                linear_branch(1)
+        for p in range(1, PIECES):
+            values_of_piece(p)
+            if p >= 2:
+                turn(p - 2)
+                weigh(p - 2)
+        turn_back(0)
+        turn_back(1)
+        linear_branch(1)
+        turn(HALVES - 2)
+        weigh(HALVES - 2)
+        turn_back(2)
+        turn(HALVES - 1)
+        weigh(HALVES - 1)
+        for u in range(3, HALVES):
+            turn_back(u)
 
         for bank, columns in zip(out_banks, out_columns):
             nc.scalar.activation(result[:, columns], bank[:, columns], ACT.Gelu, bias=bias_res)

@@ -21,6 +21,7 @@ BLOCK = 128
 BLOCKS = S // BLOCK
 PER_BLOCK = BLOCK // NODES
 PER_BANK = 4
+HELPED = 2
 HALVES = BLOCKS * K // PER_BANK
 
 FLOPS = 2 * C * (2 * C) * N + 2 * C * (2 * C) * S + 2 * C * C * N
@@ -138,6 +139,8 @@ def tile_attnno_kernel(tc, x, wkv, wqr, bqr, same_head, offs, out):
             for t in range(PER_BANK):
                 nc.tensor.transpose(turned_view(u)[:, t, :], val[:, b, first + t, :], identity[:])
 
+        terms_of = {}
+
         def weigh(u):
             b, first = u // 2, (u % 2) * PER_BANK
             part = share[:, b, :, first : first + PER_BANK]
@@ -147,16 +150,22 @@ def tile_attnno_kernel(tc, x, wkv, wqr, bqr, same_head, offs, out):
                 part.rearrange("n g t -> n t g").unsqueeze(3).to_broadcast([BLOCK, PER_BANK, HEADS, DH]),
                 ALU.mult,
             )
+            terms_of[u] = [weighted[:, u, t, :] for t in range(PER_BANK)]
+            if b < HELPED and first:
+                four = held.tile([BLOCK, PER_BANK, C], F32, name="four%d" % b)
+                nc.gpsimd.tensor_tensor(four[:], weighted[:, u - 1], weighted[:, u], ALU.add)
+                terms_of[u - 1] = []
+                terms_of[u] = [four[:, t, :] for t in range(PER_BANK)]
 
         out_columns = [slice(0, S - BLOCK), slice(S - BLOCK, S)]
 
         def turn_back(u):
             b = u // 2
             bank = out_banks[b // (BLOCKS - 1)]
-            for t in range(PER_BANK):
+            for t, term in enumerate(terms_of[u]):
                 nc.tensor.matmul(
-                    bank[:, b * BLOCK : (b + 1) * BLOCK], weighted[:, u, t, :], identity[:],
-                    start=False, stop=(u in (HALVES - 3, HALVES - 1) and t == PER_BANK - 1), is_transpose=True,
+                    bank[:, b * BLOCK : (b + 1) * BLOCK], term, identity[:],
+                    start=False, stop=(u in (3, HALVES - 1) and t == PER_BANK - 1), is_transpose=True,
                 )
 
         def linear_branch(i):
@@ -185,15 +194,12 @@ def tile_attnno_kernel(tc, x, wkv, wqr, bqr, same_head, offs, out):
             if p >= 2:
                 turn(p - 2)
                 weigh(p - 2)
-        turn_back(0)
         turn_back(1)
         linear_branch(1)
-        turn(HALVES - 2)
-        weigh(HALVES - 2)
-        turn_back(2)
-        turn(HALVES - 1)
-        weigh(HALVES - 1)
-        for u in range(3, HALVES):
+        for u in (HALVES - 2, HALVES - 1):
+            turn(u)
+            weigh(u)
+        for u in (4, 5, 3, 6, 7):
             turn_back(u)
 
         for bank, columns in zip(out_banks, out_columns):

@@ -22,7 +22,7 @@ BLOCKS = S // BLOCK
 PER_BLOCK = BLOCK // NODES
 PER_BANK = 4
 HELPED = 2
-HALVES = BLOCKS * K // PER_BANK
+LAST_STEP = 2
 
 FLOPS = 2 * C * (2 * C) * N + 2 * C * (2 * C) * S + 2 * C * C * N
 
@@ -58,6 +58,7 @@ def tile_attnno_kernel(tc, x, wkv, wqr, bqr, same_head, offs, out):
         score_banks = banks[1:4]
         value_banks = [banks[0]] + [(banks[7], banks[1], banks[2])[i % 3] for i in range(PIECES - 1)]
         turned_banks = [banks[0], banks[4], banks[6], banks[3]]
+        last_banks = [banks[6], banks[3], banks[1], banks[2]]
         out_banks = [banks[5], banks[7]]
 
         h = held.tile([C, S], BF16, name="h")
@@ -68,7 +69,7 @@ def tile_attnno_kernel(tc, x, wkv, wqr, bqr, same_head, offs, out):
         q = held.tile([C, S], F32, name="q")
         prod = held.tile([C, K, S], BF16, name="prod")
         val = held.tile([C, BLOCKS, K, BLOCK], F32, name="val")
-        weighted = held.tile([BLOCK, HALVES, PER_BANK, C], F32, name="weighted")
+        weighted = held.tile([BLOCK, BLOCKS, K, C], F32, name="weighted")
         result = held.tile([C, S], F32, name="result")
 
         def nodes_of(p):
@@ -88,7 +89,7 @@ def tile_attnno_kernel(tc, x, wkv, wqr, bqr, same_head, offs, out):
         def values_of_piece(p):
             value = gathered(value_banks[p], slice(C, 2 * C), p)
             b, k = divmod(p, PER_BLOCK)
-            step = PER_BANK if p == PIECES - 1 else K
+            step = LAST_STEP if p == PIECES - 1 else K
             for first in range(0, K, step):
                 part = slice(first, first + step)
                 nc.scalar.copy(val[:, b, part, k * NODES : (k + 1) * NODES], value[:, part, :])
@@ -131,41 +132,32 @@ def tile_attnno_kernel(tc, x, wkv, wqr, bqr, same_head, offs, out):
                 share[:, blocks], share[:, blocks], rden[:, blocks].unsqueeze(3).to_broadcast(shape), ALU.mult
             )
 
-        def turned_view(u):
-            return turned_banks[u % len(turned_banks)][:].rearrange("n (t c) -> n t c", c=C)
-
-        def turn(u):
-            b, first = u // 2, (u % 2) * PER_BANK
-            for t in range(PER_BANK):
-                nc.tensor.transpose(turned_view(u)[:, t, :], val[:, b, first + t, :], identity[:])
-
-        terms_of = {}
-
-        def weigh(u):
-            b, first = u // 2, (u % 2) * PER_BANK
-            part = share[:, b, :, first : first + PER_BANK]
+        def turn_and_weigh(b, part, bank):
+            count = part.stop - part.start
+            turned = bank[:, 0 : count * C].rearrange("n (t c) -> n t c", c=C)
+            for t in range(count):
+                nc.tensor.transpose(turned[:, t, :], val[:, b, part.start + t, :], identity[:])
             nc.vector.tensor_tensor(
-                weighted[:, u].rearrange("n t (g d) -> n t g d", d=DH),
-                turned_view(u).rearrange("n t (g d) -> n t g d", d=DH),
-                part.rearrange("n g t -> n t g").unsqueeze(3).to_broadcast([BLOCK, PER_BANK, HEADS, DH]),
+                weighted[:, b, part].rearrange("n t (g d) -> n t g d", d=DH),
+                turned.rearrange("n t (g d) -> n t g d", d=DH),
+                share[:, b, :, part].rearrange("n g t -> n t g").unsqueeze(3).to_broadcast([BLOCK, count, HEADS, DH]),
                 ALU.mult,
             )
-            terms_of[u] = [weighted[:, u, t, :] for t in range(PER_BANK)]
-            if b < HELPED and first:
-                four = held.tile([BLOCK, PER_BANK, C], F32, name="four%d" % b)
-                nc.gpsimd.tensor_tensor(four[:], weighted[:, u - 1], weighted[:, u], ALU.add)
-                terms_of[u - 1] = []
-                terms_of[u] = [four[:, t, :] for t in range(PER_BANK)]
+
+        def halved(b):
+            four = held.tile([BLOCK, PER_BANK, C], F32, name="four%d" % b)
+            nc.gpsimd.tensor_tensor(four[:], weighted[:, b, 0:PER_BANK], weighted[:, b, PER_BANK:K], ALU.add)
+            return four
 
         out_columns = [slice(0, S - BLOCK), slice(S - BLOCK, S)]
 
-        def turn_back(u):
-            b = u // 2
+        def turn_back(b, terms, closes):
             bank = out_banks[b // (BLOCKS - 1)]
-            for t, term in enumerate(terms_of[u]):
+            count = terms.shape[1]
+            for t in range(count):
                 nc.tensor.matmul(
-                    bank[:, b * BLOCK : (b + 1) * BLOCK], term, identity[:],
-                    start=False, stop=(u in (3, HALVES - 1) and t == PER_BANK - 1), is_transpose=True,
+                    bank[:, b * BLOCK : (b + 1) * BLOCK], terms[:, t, :], identity[:],
+                    start=False, stop=(closes and t == count - 1), is_transpose=True,
                 )
 
         def linear_branch(i):
@@ -189,18 +181,22 @@ def tile_attnno_kernel(tc, x, wkv, wqr, bqr, same_head, offs, out):
             for group in range(len(groups)):
                 stage(group)
 
+        four_of = []
         for p in range(1, PIECES):
             values_of_piece(p)
             if p >= 2:
-                turn(p - 2)
-                weigh(p - 2)
-        turn_back(1)
+                b, k = divmod(p - 2, PER_BLOCK)
+                turn_and_weigh(b, slice(k * PER_BANK, (k + 1) * PER_BANK), turned_banks[(p - 2) % len(turned_banks)])
+                if b < HELPED and k:
+                    four_of.append(halved(b))
+        last = BLOCKS - 1
+        turn_back(0, four_of[0][:], False)
+        for i, bank in enumerate(last_banks):
+            turn_and_weigh(last, slice(i * LAST_STEP, (i + 1) * LAST_STEP), bank)
         linear_branch(1)
-        for u in (HALVES - 2, HALVES - 1):
-            turn(u)
-            weigh(u)
-        for u in (4, 5, 3, 6, 7):
-            turn_back(u)
+        turn_back(2, weighted[:, 2], False)
+        turn_back(1, four_of[1][:], True)
+        turn_back(last, weighted[:, last], True)
 
         for bank, columns in zip(out_banks, out_columns):
             nc.scalar.activation(result[:, columns], bank[:, columns], ACT.Gelu, bias=bias_res)

@@ -21,7 +21,7 @@ BLOCK = 128
 BLOCKS = S // BLOCK
 PER_BLOCK = BLOCK // NODES
 PER_BANK = 4
-HELPED = 2
+HELPED = (2, 3, 4)
 LAST_STEP = 2
 
 FLOPS = 2 * C * (2 * C) * N + 2 * C * (2 * C) * S + 2 * C * C * N
@@ -144,10 +144,11 @@ def tile_attnno_kernel(tc, x, wkv, wqr, bqr, same_head, offs, out):
                 ALU.mult,
             )
 
-        def halved(b):
-            four = held.tile([BLOCK, PER_BANK, C], F32, name="four%d" % b)
-            nc.gpsimd.tensor_tensor(four[:], weighted[:, b, 0:PER_BANK], weighted[:, b, PER_BANK:K], ALU.add)
-            return four
+        def halved(u):
+            b, first = u // 2, (u % 2) * PER_BANK
+            two = held.tile([BLOCK, 2, C], F32, name="two%d" % u)
+            nc.gpsimd.tensor_tensor(two[:], weighted[:, b, first : first + 2], weighted[:, b, first + 2 : first + 4], ALU.add)
+            return two
 
         out_columns = [slice(0, S - BLOCK), slice(S - BLOCK, S)]
 
@@ -181,21 +182,27 @@ def tile_attnno_kernel(tc, x, wkv, wqr, bqr, same_head, offs, out):
             for group in range(len(groups)):
                 stage(group)
 
-        four_of = []
+        terms_of = []
+
+        def weigh_half(u):
+            b, k = divmod(u, PER_BLOCK)
+            part = slice(k * PER_BANK, (k + 1) * PER_BANK)
+            turn_and_weigh(b, part, turned_banks[u % len(turned_banks)])
+            terms_of.append(halved(u)[:] if u in HELPED else weighted[:, b, part])
+
         for p in range(1, PIECES):
             values_of_piece(p)
-            if p >= 2:
-                b, k = divmod(p - 2, PER_BLOCK)
-                turn_and_weigh(b, slice(k * PER_BANK, (k + 1) * PER_BANK), turned_banks[(p - 2) % len(turned_banks)])
-                if b < HELPED and k:
-                    four_of.append(halved(b))
+            if p >= PIECES - 2:
+                turn_back(0, terms_of[p - (PIECES - 2)], False)
+            if p >= 3 and p % 2:
+                weigh_half(p - 3)
+                weigh_half(p - 2)
         last = BLOCKS - 1
-        turn_back(0, four_of[0][:], False)
         for i, bank in enumerate(last_banks):
             turn_and_weigh(last, slice(i * LAST_STEP, (i + 1) * LAST_STEP), bank)
         linear_branch(1)
-        turn_back(2, weighted[:, 2], False)
-        turn_back(1, four_of[1][:], True)
+        for u in (2, 3, 5, 4):
+            turn_back(u // 2, terms_of[u], u == 4)
         turn_back(last, weighted[:, last], True)
 
         for bank, columns in zip(out_banks, out_columns):

@@ -89,7 +89,7 @@ def tile_attnno_kernel(tc, x, wkv, wqr, bqr, same_head, offs, out):
         def values_of_piece(p):
             value = gathered(value_banks[p], slice(C, 2 * C), p)
             b, k = divmod(p, PER_BLOCK)
-            step = LAST_STEP if p == PIECES - 1 else K
+            step = LAST_STEP if p == PIECES - 1 else PER_BANK if k else K
             for first in range(0, K, step):
                 part = slice(first, first + step)
                 nc.scalar.copy(val[:, b, part, k * NODES : (k + 1) * NODES], value[:, part, :])
@@ -192,11 +192,12 @@ def tile_attnno_kernel(tc, x, wkv, wqr, bqr, same_head, offs, out):
 
         for p in range(1, PIECES):
             values_of_piece(p)
-            if p >= PIECES - 2:
-                turn_back(0, terms_of[p - (PIECES - 2)], False)
+            if p == PIECES - 2:
+                turn_back(0, terms_of[0], False)
             if p >= 3 and p % 2:
                 weigh_half(p - 3)
                 weigh_half(p - 2)
+        turn_back(0, terms_of[1], False)
         last = BLOCKS - 1
         for i, bank in enumerate(last_banks):
             turn_and_weigh(last, slice(i * LAST_STEP, (i + 1) * LAST_STEP), bank)

@@ -21,7 +21,7 @@ BLOCK = 128
 BLOCKS = S // BLOCK
 PER_BLOCK = BLOCK // NODES
 PER_BANK = 4
-HELPED = (2, 3, 4)
+HELPED = (0, 1, 2, 3, 4)
 LAST_STEP = 2
 
 FLOPS = 2 * C * (2 * C) * N + 2 * C * (2 * C) * S + 2 * C * C * N
@@ -192,12 +192,11 @@ def tile_attnno_kernel(tc, x, wkv, wqr, bqr, same_head, offs, out):
 
         for p in range(1, PIECES):
             values_of_piece(p)
-            if p == PIECES - 2:
-                turn_back(0, terms_of[0], False)
             if p >= 3 and p % 2:
                 weigh_half(p - 3)
                 weigh_half(p - 2)
-        turn_back(0, terms_of[1], False)
+        for u in (0, 1):
+            turn_back(0, terms_of[u], False)
         last = BLOCKS - 1
         for i, bank in enumerate(last_banks):
             turn_and_weigh(last, slice(i * LAST_STEP, (i + 1) * LAST_STEP), bank)

@@ -62,9 +62,9 @@ def tile_attnno_kernel(tc, x, wkv, wqr, bqr, same_head, offs, out):
         out_banks = [banks[5], banks[7]]
 
         h = held.tile([C, S], BF16, name="h")
-        halves = (slice(0, S // 2), slice(S // 2, S))
-        for half in halves:
-            nc.scalar.activation(h[:, half], x_sb[:, half], ACT.Gelu)
+        quarters = [slice(b * BLOCK, (b + 1) * BLOCK) for b in range(BLOCKS)]
+        for columns in quarters:
+            nc.scalar.activation(h[:, columns], x_sb[:, columns], ACT.Gelu)
 
         q = held.tile([C, S], F32, name="q")
         prod = held.tile([C, K, S], BF16, name="prod")
@@ -152,21 +152,22 @@ def tile_attnno_kernel(tc, x, wkv, wqr, bqr, same_head, offs, out):
 
         out_columns = [slice(0, S - BLOCK), slice(S - BLOCK, S)]
 
-        def turn_back(b, terms, closes):
+        def turn_back(b, terms, closes, opens=False):
             bank = out_banks[b // (BLOCKS - 1)]
             count = terms.shape[1]
             for t in range(count):
                 nc.tensor.matmul(
                     bank[:, b * BLOCK : (b + 1) * BLOCK], terms[:, t, :], identity[:],
-                    start=False, stop=(closes and t == count - 1), is_transpose=True,
+                    start=(opens and t == 0), stop=(closes and t == count - 1), is_transpose=True,
                 )
 
-        def linear_branch(i):
+        def linear_branch(i, opens):
             columns = out_columns[i]
-            nc.tensor.matmul(out_banks[i][:, columns], wqr_sb[:, C : 2 * C], h[:, columns], start=True, stop=False)
+            nc.tensor.matmul(out_banks[i][:, columns], wqr_sb[:, C : 2 * C], h[:, columns], start=opens, stop=False)
 
-        for bank, half in zip(query_banks, halves):
-            nc.tensor.matmul(bank[:, half], wqr_sb[:, 0:C], h[:, half], start=True, stop=True)
+        for b, columns in enumerate(quarters):
+            nc.tensor.matmul(query_banks[b // 2][:, columns], wqr_sb[:, 0:C], h[:, columns], start=True, stop=True)
+        for bank, half in zip(query_banks, (slice(0, S // 2), slice(S // 2, S))):
             nc.scalar.activation(q[:, half], bank[:, half], ACT.Identity, bias=bias_q)
         exp_table = held.tile([C, 1], F32, name="exp_table")
         nc.scalar.activation(exp_table[:], q[:, S - 1 : S], ACT.Exp, scale=0.0)
@@ -176,7 +177,6 @@ def tile_attnno_kernel(tc, x, wkv, wqr, bqr, same_head, offs, out):
         values_of_piece(0)
         scores(0)
         scores(1)
-        linear_branch(0)
         scores(2)
         for stage in (exponentials, normalise):
             for group in range(len(groups)):
@@ -196,13 +196,15 @@ def tile_attnno_kernel(tc, x, wkv, wqr, bqr, same_head, offs, out):
                 weigh_half(p - 3)
                 weigh_half(p - 2)
         for u in (0, 1):
-            turn_back(0, terms_of[u], False)
+            turn_back(0, terms_of[u], False, opens=(u == 0))
         last = BLOCKS - 1
         for i, bank in enumerate(last_banks):
             turn_and_weigh(last, slice(i * LAST_STEP, (i + 1) * LAST_STEP), bank)
-        linear_branch(1)
-        for u in (2, 3, 5, 4):
-            turn_back(u // 2, terms_of[u], u == 4)
+        linear_branch(1, True)
+        for u in (2, 3, 5):
+            turn_back(u // 2, terms_of[u], False)
+        linear_branch(0, False)
+        turn_back(2, terms_of[4], True)
         turn_back(last, weighted[:, last], True)
 
         for bank, columns in zip(out_banks, out_columns):

@@ -58,8 +58,8 @@ def tile_attnno_kernel(tc, x, wkv, wqr, bqr, same_head, offs, out):
         score_banks = banks[1:4]
         value_banks = [banks[0]] + [(banks[7], banks[1], banks[2])[i % 3] for i in range(PIECES - 1)]
         turned_banks = [banks[0], banks[4], banks[6], banks[3]]
-        last_banks = [banks[6], banks[3], banks[1], banks[2]]
-        out_banks = [banks[5], banks[7]]
+        last_banks = [banks[6], banks[3], banks[1], banks[5]]
+        out_banks = [banks[2], banks[7]]
 
         h = held.tile([C, S], BF16, name="h")
         quarters = [slice(b * BLOCK, (b + 1) * BLOCK) for b in range(BLOCKS)]
@@ -195,15 +195,16 @@ def tile_attnno_kernel(tc, x, wkv, wqr, bqr, same_head, offs, out):
             if p >= 3 and p % 2:
                 weigh_half(p - 3)
                 weigh_half(p - 2)
-        for u in (0, 1):
-            turn_back(0, terms_of[u], False, opens=(u == 0))
+        linear_branch(0, True)
+        nc.tensor.matmul(out_banks[0][:, 0:BLOCK], terms_of[0][:, 0, :], identity[:], start=False, stop=False)
+        turn_back(0, terms_of[0][:, 1:2, :], False)
+        turn_back(0, terms_of[1], False)
         last = BLOCKS - 1
         for i, bank in enumerate(last_banks):
             turn_and_weigh(last, slice(i * LAST_STEP, (i + 1) * LAST_STEP), bank)
         linear_branch(1, True)
         for u in (2, 3, 5):
             turn_back(u // 2, terms_of[u], False)
-        linear_branch(0, False)
         turn_back(2, terms_of[4], True)
         turn_back(last, weighted[:, last], True)
 

@@ -152,18 +152,18 @@ def tile_attnno_kernel(tc, x, wkv, wqr, bqr, same_head, offs, out):
 
         out_columns = [slice(0, S - BLOCK), slice(S - BLOCK, S)]
 
-        def turn_back(b, terms, closes, opens=False):
+        def turn_back(b, terms, closes):
             bank = out_banks[b // (BLOCKS - 1)]
             count = terms.shape[1]
             for t in range(count):
                 nc.tensor.matmul(
                     bank[:, b * BLOCK : (b + 1) * BLOCK], terms[:, t, :], identity[:],
-                    start=(opens and t == 0), stop=(closes and t == count - 1), is_transpose=True,
+                    start=False, stop=(closes and t == count - 1), is_transpose=True,
                 )
 
-        def linear_branch(i, opens):
+        def linear_branch(i):
             columns = out_columns[i]
-            nc.tensor.matmul(out_banks[i][:, columns], wqr_sb[:, C : 2 * C], h[:, columns], start=opens, stop=False)
+            nc.tensor.matmul(out_banks[i][:, columns], wqr_sb[:, C : 2 * C], h[:, columns], start=True, stop=False)
 
         for b, columns in enumerate(quarters):
             nc.tensor.matmul(query_banks[b // 2][:, columns], wqr_sb[:, 0:C], h[:, columns], start=True, stop=True)
@@ -195,14 +195,13 @@ def tile_attnno_kernel(tc, x, wkv, wqr, bqr, same_head, offs, out):
             if p >= 3 and p % 2:
                 weigh_half(p - 3)
                 weigh_half(p - 2)
-        linear_branch(0, True)
-        nc.tensor.matmul(out_banks[0][:, 0:BLOCK], terms_of[0][:, 0, :], identity[:], start=False, stop=False)
-        turn_back(0, terms_of[0][:, 1:2, :], False)
-        turn_back(0, terms_of[1], False)
+        linear_branch(0)
+        for u in (0, 1):
+            turn_back(0, terms_of[u], False)
         last = BLOCKS - 1
         for i, bank in enumerate(last_banks):
             turn_and_weigh(last, slice(i * LAST_STEP, (i + 1) * LAST_STEP), bank)
-        linear_branch(1, True)
+        linear_branch(1)
         for u in (2, 3, 5):
             turn_back(u // 2, terms_of[u], False)
         turn_back(2, terms_of[4], True)

@@ -22,7 +22,9 @@ BLOCKS = S // BLOCK
 PER_BLOCK = BLOCK // NODES
 PER_BANK = 4
 HELPED = (0, 1, 2, 3, 4)
-LAST_STEP = 2
+BEHIND_RUN = 4
+FIRST_STEP = 2
+LAST_STEPS = (2, 2, 3, 1)
 
 FLOPS = 2 * C * (2 * C) * N + 2 * C * (2 * C) * S + 2 * C * C * N
 
@@ -46,7 +48,7 @@ def tile_attnno_kernel(tc, x, wkv, wqr, bqr, same_head, offs, out):
         nc.sync.dma_start(offsets[:], offs)
         nc.sync.dma_start(wkv_sb[:], wkv)
         nc.sync.dma_start(biases[:], bqr.rearrange("(a p) o -> p (a o)", p=C))
-        nc.sync.dma_start(head_sb[:], same_head)
+        nc.gpsimd.dma_start(head_sb[:], same_head)
 
         identity = held.tile([BLOCK, BLOCK], F32, name="identity")
         make_identity(nc, identity[:])
@@ -58,8 +60,8 @@ def tile_attnno_kernel(tc, x, wkv, wqr, bqr, same_head, offs, out):
         score_banks = banks[1:4]
         value_banks = [banks[0]] + [(banks[7], banks[1], banks[2])[i % 3] for i in range(PIECES - 1)]
         turned_banks = [banks[0], banks[4], banks[6], banks[3]]
-        last_banks = [banks[6], banks[3], banks[1], banks[5]]
-        out_banks = [banks[2], banks[7]]
+        last_banks = [banks[6], banks[3], banks[2], banks[5]]
+        out_banks = [banks[1], banks[0], banks[7]]
 
         h = held.tile([C, S], BF16, name="h")
         quarters = [slice(b * BLOCK, (b + 1) * BLOCK) for b in range(BLOCKS)]
@@ -75,6 +77,11 @@ def tile_attnno_kernel(tc, x, wkv, wqr, bqr, same_head, offs, out):
         def nodes_of(p):
             return slice(p * NODES, (p + 1) * NODES)
 
+        def parts_of(steps):
+            return [slice(sum(steps[:i]), sum(steps[: i + 1])) for i in range(len(steps))]
+
+        last_parts = parts_of(LAST_STEPS)
+
         def gathered(bank, weight_columns, p):
             picked = h[:].indirect(offsets[:, p * (PIECE // 16) : (p + 1) * (PIECE // 16)])
             nc.tensor.matmul(bank[:], wkv_sb[:, weight_columns], picked, start=True, stop=True)
@@ -89,9 +96,7 @@ def tile_attnno_kernel(tc, x, wkv, wqr, bqr, same_head, offs, out):
         def values_of_piece(p):
             value = gathered(value_banks[p], slice(C, 2 * C), p)
             b, k = divmod(p, PER_BLOCK)
-            step = LAST_STEP if p == PIECES - 1 else PER_BANK if k else K
-            for first in range(0, K, step):
-                part = slice(first, first + step)
+            for part in last_parts if p == PIECES - 1 else parts_of([PER_BANK, PER_BANK] if k else [K]):
                 nc.scalar.copy(val[:, b, part, k * NODES : (k + 1) * NODES], value[:, part, :])
 
         groups = [range(0, 1), range(1, 2), range(2, BLOCKS)]
@@ -150,10 +155,10 @@ def tile_attnno_kernel(tc, x, wkv, wqr, bqr, same_head, offs, out):
             nc.gpsimd.tensor_tensor(two[:], weighted[:, b, first : first + 2], weighted[:, b, first + 2 : first + 4], ALU.add)
             return two
 
-        out_columns = [slice(0, S - BLOCK), slice(S - BLOCK, S)]
+        out_columns = [slice(0, 2 * BLOCK), slice(2 * BLOCK, 3 * BLOCK), slice(3 * BLOCK, S)]
 
         def turn_back(b, terms, closes):
-            bank = out_banks[b // (BLOCKS - 1)]
+            bank = out_banks[max(b - 1, 0)]
             count = terms.shape[1]
             for t in range(count):
                 nc.tensor.matmul(
@@ -187,7 +192,11 @@ def tile_attnno_kernel(tc, x, wkv, wqr, bqr, same_head, offs, out):
         def weigh_half(u):
             b, k = divmod(u, PER_BLOCK)
             part = slice(k * PER_BANK, (k + 1) * PER_BANK)
-            turn_and_weigh(b, part, turned_banks[u % len(turned_banks)])
+            if u == BEHIND_RUN:
+                turn_and_weigh(b, slice(part.start, part.start + FIRST_STEP), last_banks[-1])
+                turn_and_weigh(b, slice(part.start + FIRST_STEP, part.stop), turned_banks[u % len(turned_banks)])
+            else:
+                turn_and_weigh(b, part, turned_banks[u % len(turned_banks)])
             terms_of.append(halved(u)[:] if u in HELPED else weighted[:, b, part])
 
         for p in range(1, PIECES):
@@ -196,16 +205,20 @@ def tile_attnno_kernel(tc, x, wkv, wqr, bqr, same_head, offs, out):
                 weigh_half(p - 3)
                 weigh_half(p - 2)
         linear_branch(0)
+        last = BLOCKS - 1
         for u in (0, 1):
             turn_back(0, terms_of[u], False)
-        last = BLOCKS - 1
         for i, bank in enumerate(last_banks):
-            turn_and_weigh(last, slice(i * LAST_STEP, (i + 1) * LAST_STEP), bank)
+            if i == 2:
+                turn_back(1, terms_of[2], False)
+            turn_and_weigh(last, last_parts[i], bank)
+        turn_back(1, terms_of[3], True)
         linear_branch(1)
-        for u in (2, 3, 5):
-            turn_back(u // 2, terms_of[u], False)
+        linear_branch(2)
+        turn_back(2, terms_of[5], False)
+        turn_back(last, weighted[:, last, : LAST_STEPS[0]], False)
         turn_back(2, terms_of[4], True)
-        turn_back(last, weighted[:, last], True)
+        turn_back(last, weighted[:, last, LAST_STEPS[0] :], True)
 
         for bank, columns in zip(out_banks, out_columns):
             nc.scalar.activation(result[:, columns], bank[:, columns], ACT.Gelu, bias=bias_res)

@@ -80,6 +80,7 @@ def tile_attnno_kernel(tc, x, wkv, wqr, bqr, same_head, offs, out):
         def parts_of(steps):
             return [slice(sum(steps[:i]), sum(steps[: i + 1])) for i in range(len(steps))]
 
+        halves = parts_of([PER_BANK, PER_BANK])
         last_parts = parts_of(LAST_STEPS)
 
         def gathered(bank, weight_columns, p):
@@ -96,7 +97,7 @@ def tile_attnno_kernel(tc, x, wkv, wqr, bqr, same_head, offs, out):
         def values_of_piece(p):
             value = gathered(value_banks[p], slice(C, 2 * C), p)
             b, k = divmod(p, PER_BLOCK)
-            for part in last_parts if p == PIECES - 1 else parts_of([PER_BANK, PER_BANK] if k else [K]):
+            for part in last_parts if p == PIECES - 1 else halves if k else [slice(0, K)]:
                 nc.scalar.copy(val[:, b, part, k * NODES : (k + 1) * NODES], value[:, part, :])
 
         groups = [range(0, 1), range(1, 2), range(2, BLOCKS)]
@@ -212,13 +213,13 @@ def tile_attnno_kernel(tc, x, wkv, wqr, bqr, same_head, offs, out):
             if i == 2:
                 turn_back(1, terms_of[2], False)
             turn_and_weigh(last, last_parts[i], bank)
-        turn_back(1, terms_of[3], True)
         linear_branch(1)
         linear_branch(2)
         turn_back(2, terms_of[5], False)
-        turn_back(last, weighted[:, last, : LAST_STEPS[0]], False)
+        turn_back(1, terms_of[3], True)
+        turn_back(last, weighted[:, last, halves[0]], False)
         turn_back(2, terms_of[4], True)
-        turn_back(last, weighted[:, last, LAST_STEPS[0] :], True)
+        turn_back(last, weighted[:, last, halves[1]], True)
 
         for bank, columns in zip(out_banks, out_columns):
             nc.scalar.activation(result[:, columns], bank[:, columns], ACT.Gelu, bias=bias_res)

@@ -202,10 +202,11 @@ def tile_attnno_kernel(tc, x, wkv, wqr, bqr, same_head, offs, out):
 
         for p in range(1, PIECES):
             values_of_piece(p)
+            if p == PIECES - 1:
+                linear_branch(0)
             if p >= 3 and p % 2:
                 weigh_half(p - 3)
                 weigh_half(p - 2)
-        linear_branch(0)
         last = BLOCKS - 1
         for u in (0, 1):
             turn_back(0, terms_of[u], False)

@@ -24,7 +24,7 @@ PER_BANK = 4
 HELPED = (0, 1, 2, 3, 4)
 BEHIND_RUN = 4
 FIRST_STEP = 2
-LAST_STEPS = (2, 2, 3, 1)
+LAST_STEPS = (4, 3, 1)
 
 FLOPS = 2 * C * (2 * C) * N + 2 * C * (2 * C) * S + 2 * C * C * N
 
@@ -60,7 +60,7 @@ def tile_attnno_kernel(tc, x, wkv, wqr, bqr, same_head, offs, out):
         score_banks = banks[1:4]
         value_banks = [banks[0]] + [(banks[7], banks[1], banks[2])[i % 3] for i in range(PIECES - 1)]
         turned_banks = [banks[0], banks[4], banks[6], banks[3]]
-        last_banks = [banks[6], banks[3], banks[2], banks[5]]
+        last_banks = [banks[6], banks[3], banks[5]]
         out_banks = [banks[1], banks[0], banks[7]]
 
         h = held.tile([C, S], BF16, name="h")
@@ -208,11 +208,8 @@ def tile_attnno_kernel(tc, x, wkv, wqr, bqr, same_head, offs, out):
                 weigh_half(p - 3)
                 weigh_half(p - 2)
         last = BLOCKS - 1
-        for u in (0, 1):
-            turn_back(0, terms_of[u], False)
         for i, bank in enumerate(last_banks):
-            if i == 2:
-                turn_back(1, terms_of[2], False)
+            turn_back(i // 2, terms_of[i], False)
             turn_and_weigh(last, last_parts[i], bank)
         linear_branch(1)
         linear_branch(2)

@@ -48,7 +48,7 @@ def tile_attnno_kernel(tc, x, wkv, wqr, bqr, same_head, offs, out):
         nc.sync.dma_start(offsets[:], offs)
         nc.sync.dma_start(wkv_sb[:], wkv)
         nc.sync.dma_start(biases[:], bqr.rearrange("(a p) o -> p (a o)", p=C))
-        nc.gpsimd.dma_start(head_sb[:], same_head)
+        nc.sync.dma_start(head_sb[:], same_head)
 
         identity = held.tile([BLOCK, BLOCK], F32, name="identity")
         make_identity(nc, identity[:])
@@ -61,7 +61,7 @@ def tile_attnno_kernel(tc, x, wkv, wqr, bqr, same_head, offs, out):
         value_banks = [banks[0]] + [(banks[7], banks[1], banks[2])[i % 3] for i in range(PIECES - 1)]
         turned_banks = [banks[0], banks[4], banks[6], banks[3]]
         last_banks = [banks[6], banks[3], banks[5]]
-        out_banks = [banks[1], banks[0], banks[7]]
+        out_banks = [banks[1], banks[7]]
 
         h = held.tile([C, S], BF16, name="h")
         quarters = [slice(b * BLOCK, (b + 1) * BLOCK) for b in range(BLOCKS)]
@@ -156,10 +156,10 @@ def tile_attnno_kernel(tc, x, wkv, wqr, bqr, same_head, offs, out):
             nc.gpsimd.tensor_tensor(two[:], weighted[:, b, first : first + 2], weighted[:, b, first + 2 : first + 4], ALU.add)
             return two
 
-        out_columns = [slice(0, 2 * BLOCK), slice(2 * BLOCK, 3 * BLOCK), slice(3 * BLOCK, S)]
+        out_columns = [slice(0, S - BLOCK), slice(S - BLOCK, S)]
 
         def turn_back(b, terms, closes):
-            bank = out_banks[max(b - 1, 0)]
+            bank = out_banks[b // (BLOCKS - 1)]
             count = terms.shape[1]
             for t in range(count):
                 nc.tensor.matmul(
@@ -212,12 +212,9 @@ def tile_attnno_kernel(tc, x, wkv, wqr, bqr, same_head, offs, out):
             turn_back(i // 2, terms_of[i], False)
             turn_and_weigh(last, last_parts[i], bank)
         linear_branch(1)
-        linear_branch(2)
-        turn_back(2, terms_of[5], False)
-        turn_back(1, terms_of[3], True)
-        turn_back(last, weighted[:, last, halves[0]], False)
-        turn_back(2, terms_of[4], True)
-        turn_back(last, weighted[:, last, halves[1]], True)
+        for u in (3, 5, 4):
+            turn_back(u // 2, terms_of[u], u == 4)
+        turn_back(last, weighted[:, last], True)
 
         for bank, columns in zip(out_banks, out_columns):
             nc.scalar.activation(result[:, columns], bank[:, columns], ACT.Gelu, bias=bias_res)

@@ -39,20 +39,24 @@ def tile_attnno_kernel(tc, x, wkv, wqr, bqr, same_head, offs, out):
         x_sb = held.tile([C, S], BF16, name="x_sb")
         wkv_sb = held.tile([C, 2 * C], BF16, name="wkv_sb")
         wqr_sb = held.tile([C, 2 * C], BF16, name="wqr_sb")
-        head_sb = held.tile([C, C], BF16, name="head_sb")
         biases = held.tile([C, 2], F32, name="biases")
         bias_q = biases[:, 0:1]
         bias_res = biases[:, 1:2]
-        nc.sync.dma_start(x_sb[:], x)
+        for half in (slice(0, S // 2), slice(S // 2, S)):
+            nc.sync.dma_start(x_sb[:, half], x[:, half])
         nc.sync.dma_start(wqr_sb[:], wqr)
         nc.sync.dma_start(offsets[:], offs)
         nc.sync.dma_start(wkv_sb[:], wkv)
         nc.sync.dma_start(biases[:], bqr.rearrange("(a p) o -> p (a o)", p=C))
-        nc.sync.dma_start(head_sb[:], same_head)
 
         identity = held.tile([BLOCK, BLOCK], F32, name="identity")
         make_identity(nc, identity[:])
-        head_columns = head_sb[:].rearrange("e (g d) -> e g d", d=DH)[:, :, 0]
+        head_columns = held.tile([C, HEADS], BF16, name="head_columns")[:]
+        nc.gpsimd.memset(head_columns, 1.0)
+        for base, sign in ((0, 1), (DH - 1, -1)):
+            nc.gpsimd.affine_select(
+                head_columns, head_columns, [[-sign * DH, HEADS]], ALU.is_ge, 0.0, base=base, channel_multiplier=sign
+            )
 
         banks = [psum.tile([C, PIECE], F32, name="bank%d" % i) for i in range(8)]
         query_banks = [banks[4], banks[7]]
@@ -119,24 +123,31 @@ def tile_attnno_kernel(tc, x, wkv, wqr, bqr, same_head, offs, out):
         top = held.tile([BLOCK, BLOCKS, HEADS], F32, name="top")
         rden = held.tile([BLOCK, BLOCKS, HEADS], F32, name="rden")
 
+        def blocks_of(group):
+            return slice(groups[group].start, groups[group].stop)
+
+        def over_neighbours(per_head, group):
+            return per_head[:, blocks_of(group)].unsqueeze(3).to_broadcast([BLOCK, len(groups[group]), HEADS, K])
+
+        def maxima(group):
+            score = score_view(group).rearrange("n i t g -> n i g t")
+            nc.vector.tensor_reduce(top[:, blocks_of(group)], score, X_AXIS, ALU.max)
+
         def exponentials(group):
             score = score_view(group).rearrange("n i t g -> n i g t")
-            blocks = slice(groups[group].start, groups[group].stop)
-            shape = [BLOCK, len(groups[group]), HEADS, K]
-            nc.vector.tensor_reduce(top[:, blocks], score, X_AXIS, ALU.max)
-            nc.vector.tensor_tensor(
-                share[:, blocks], score, top[:, blocks].unsqueeze(3).to_broadcast(shape), ALU.subtract
-            )
-            nc.scalar.activation(share[:, blocks], share[:, blocks], ACT.Exp, scale=1.0 / math.sqrt(DH))
+            mine = share[:, blocks_of(group)]
+            nc.vector.tensor_tensor(mine, score, over_neighbours(top, group), ALU.subtract)
+            nc.scalar.activation(mine, mine, ACT.Exp, scale=1.0 / math.sqrt(DH))
+
+        def denominators(group):
+            nc.vector.tensor_reduce(rden[:, blocks_of(group)], share[:, blocks_of(group)], X_AXIS, ALU.add)
+
+        def reciprocals(group):
+            nc.vector.reciprocal(rden[:, blocks_of(group)], rden[:, blocks_of(group)])
 
         def normalise(group):
-            blocks = slice(groups[group].start, groups[group].stop)
-            shape = [BLOCK, len(groups[group]), HEADS, K]
-            nc.vector.tensor_reduce(rden[:, blocks], share[:, blocks], X_AXIS, ALU.add)
-            nc.vector.reciprocal(rden[:, blocks], rden[:, blocks])
-            nc.vector.tensor_tensor(
-                share[:, blocks], share[:, blocks], rden[:, blocks].unsqueeze(3).to_broadcast(shape), ALU.mult
-            )
+            mine = share[:, blocks_of(group)]
+            nc.vector.tensor_tensor(mine, mine, over_neighbours(rden, group), ALU.mult)
 
         def turn_and_weigh(b, part, bank):
             count = part.stop - part.start
@@ -184,7 +195,7 @@ def tile_attnno_kernel(tc, x, wkv, wqr, bqr, same_head, offs, out):
         scores(0)
         scores(1)
         scores(2)
-        for stage in (exponentials, normalise):
+        for stage in (maxima, exponentials, denominators, reciprocals, normalise):
             for group in range(len(groups)):
                 stage(group)
 

@@ -1,7 +1,6 @@
 import math
 
 import concourse.mybir as mybir
-from concourse.masks import make_identity
 
 BF16, F32, U16 = mybir.dt.bfloat16, mybir.dt.float32, mybir.dt.uint16
 ALU = mybir.AluOpType
@@ -50,13 +49,14 @@ def tile_attnno_kernel(tc, x, wkv, wqr, bqr, same_head, offs, out):
         nc.sync.dma_start(biases[:], bqr.rearrange("(a p) o -> p (a o)", p=C))
 
         identity = held.tile([BLOCK, BLOCK], F32, name="identity")
-        make_identity(nc, identity[:])
+        distance = held.tile([BLOCK, BLOCK], F32, name="distance")
+        nc.gpsimd.iota(distance[:], [[1, BLOCK]], base=0, channel_multiplier=-1, allow_small_or_imprecise_dtypes=True)
+        nc.gpsimd.tensor_single_scalar(identity[:], distance[:], 0.0, ALU.is_equal)
+        ends = distance[:].rearrange("e (g d) -> e g d", d=DH)
+        signs = held.tile([C, HEADS], F32, name="signs")
         head_columns = held.tile([C, HEADS], BF16, name="head_columns")[:]
-        nc.gpsimd.memset(head_columns, 1.0)
-        for base, sign in ((0, 1), (DH - 1, -1)):
-            nc.gpsimd.affine_select(
-                head_columns, head_columns, [[-sign * DH, HEADS]], ALU.is_ge, 0.0, base=base, channel_multiplier=sign
-            )
+        nc.gpsimd.tensor_tensor(signs[:], ends[:, :, 0], ends[:, :, DH - 1], ALU.mult)
+        nc.gpsimd.tensor_single_scalar(head_columns, signs[:], 0.0, ALU.is_le)
 
         banks = [psum.tile([C, PIECE], F32, name="bank%d" % i) for i in range(8)]
         query_banks = [banks[4], banks[7]]

@@ -62,9 +62,9 @@ def tile_attnno_kernel(tc, x, wkv, wqr, bqr, same_head, offs, out):
         query_banks = [banks[4], banks[7]]
         key_banks = [banks[i] for i in (0, 1, 2, 3, 5, 6, 4, 7)]
         score_banks = banks[1:4]
-        value_banks = [banks[0]] + [(banks[7], banks[1], banks[2])[i % 3] for i in range(PIECES - 1)]
-        turned_banks = [banks[0], banks[4], banks[6], banks[3]]
-        last_banks = [banks[6], banks[3], banks[5]]
+        value_banks = [banks[i] for i in (0, 7, 1, 2, 7, 1, 2, 4)]
+        turned_banks = [banks[i] for i in (0, 4, 6, 3, 0, 6)]
+        last_banks = [banks[3], banks[2], banks[5]]
         out_banks = [banks[1], banks[7]]
 
         h = held.tile([C, S], BF16, name="h")
@@ -206,15 +206,16 @@ def tile_attnno_kernel(tc, x, wkv, wqr, bqr, same_head, offs, out):
             part = slice(k * PER_BANK, (k + 1) * PER_BANK)
             if u == BEHIND_RUN:
                 turn_and_weigh(b, slice(part.start, part.start + FIRST_STEP), last_banks[-1])
-                turn_and_weigh(b, slice(part.start + FIRST_STEP, part.stop), turned_banks[u % len(turned_banks)])
+                turn_and_weigh(b, slice(part.start + FIRST_STEP, part.stop), turned_banks[u])
             else:
-                turn_and_weigh(b, part, turned_banks[u % len(turned_banks)])
+                turn_and_weigh(b, part, turned_banks[u])
             terms_of.append(halved(u)[:] if u in HELPED else weighted[:, b, part])
 
         for p in range(1, PIECES):
             values_of_piece(p)
             if p == PIECES - 1:
                 linear_branch(0)
+                linear_branch(1)
             if p >= 3 and p % 2:
                 weigh_half(p - 3)
                 weigh_half(p - 2)
@@ -222,7 +223,6 @@ def tile_attnno_kernel(tc, x, wkv, wqr, bqr, same_head, offs, out):
         for i, bank in enumerate(last_banks):
             turn_back(i // 2, terms_of[i], False)
             turn_and_weigh(last, last_parts[i], bank)
-        linear_branch(1)
         for u in (3, 5, 4):
             turn_back(u // 2, terms_of[u], u == 4)
         turn_back(last, weighted[:, last], True)

@@ -59,13 +59,16 @@ def tile_attnno_kernel(tc, x, wkv, wqr, bqr, same_head, offs, out):
         nc.gpsimd.tensor_single_scalar(head_columns, signs[:], 0.0, ALU.is_le)
 
         banks = [psum.tile([C, PIECE], F32, name="bank%d" % i) for i in range(8)]
-        query_banks = [banks[4], banks[7]]
-        key_banks = [banks[i] for i in (0, 1, 2, 3, 5, 6, 4, 7)]
-        score_banks = banks[1:4]
-        value_banks = [banks[i] for i in (0, 7, 1, 2, 7, 1, 2, 4)]
-        turned_banks = [banks[i] for i in (0, 4, 6, 3, 0, 6)]
-        last_banks = [banks[3], banks[2], banks[5]]
-        out_banks = [banks[1], banks[7]]
+        query_banks = banks[6:8]
+        key_banks = banks
+        score_banks = key_banks[1:4]
+        value_banks = [key_banks[0], key_banks[7], score_banks[0], score_banks[1]]
+        value_banks += value_banks[1:4]
+        turned_banks = [value_banks[0], key_banks[6], key_banks[5], score_banks[2]]
+        turned_banks += turned_banks[0:4:2]
+        value_banks.append(turned_banks[1])
+        last_banks = [turned_banks[3], value_banks[6], key_banks[4]]
+        out_banks = [value_banks[5], value_banks[4]]
 
         h = held.tile([C, S], BF16, name="h")
         quarters = [slice(b * BLOCK, (b + 1) * BLOCK) for b in range(BLOCKS)]

@@ -23,7 +23,8 @@ PER_BANK = 4
 HELPED = (0, 1, 2, 3, 4)
 BEHIND_RUN = 4
 FIRST_STEP = 2
-LAST_STEPS = (4, 3, 1)
+LAST_STEPS = (4, 2, 1, 1)
+COPY_STEPS = (4, 3, 1)
 
 FLOPS = 2 * C * (2 * C) * N + 2 * C * (2 * C) * S + 2 * C * C * N
 
@@ -67,7 +68,7 @@ def tile_attnno_kernel(tc, x, wkv, wqr, bqr, same_head, offs, out):
         turned_banks = [value_banks[0], key_banks[6], key_banks[5], score_banks[2]]
         turned_banks += turned_banks[0:4:2]
         value_banks.append(turned_banks[1])
-        last_banks = [turned_banks[3], value_banks[6], key_banks[4]]
+        last_banks = [turned_banks[3], value_banks[6], key_banks[4], value_banks[7]]
         out_banks = [value_banks[5], value_banks[4]]
 
         h = held.tile([C, S], BF16, name="h")
@@ -104,7 +105,7 @@ def tile_attnno_kernel(tc, x, wkv, wqr, bqr, same_head, offs, out):
         def values_of_piece(p):
             value = gathered(value_banks[p], slice(C, 2 * C), p)
             b, k = divmod(p, PER_BLOCK)
-            for part in last_parts if p == PIECES - 1 else halves if k else [slice(0, K)]:
+            for part in parts_of(COPY_STEPS) if p == PIECES - 1 else halves if k else [slice(0, K)]:
                 nc.scalar.copy(val[:, b, part, k * NODES : (k + 1) * NODES], value[:, part, :])
 
         groups = [range(0, 1), range(1, 2), range(2, BLOCKS)]
@@ -208,7 +209,7 @@ def tile_attnno_kernel(tc, x, wkv, wqr, bqr, same_head, offs, out):
             b, k = divmod(u, PER_BLOCK)
             part = slice(k * PER_BANK, (k + 1) * PER_BANK)
             if u == BEHIND_RUN:
-                turn_and_weigh(b, slice(part.start, part.start + FIRST_STEP), last_banks[-1])
+                turn_and_weigh(b, slice(part.start, part.start + FIRST_STEP), last_banks[2])
                 turn_and_weigh(b, slice(part.start + FIRST_STEP, part.stop), turned_banks[u])
             else:
                 turn_and_weigh(b, part, turned_banks[u])
@@ -224,7 +225,8 @@ def tile_attnno_kernel(tc, x, wkv, wqr, bqr, same_head, offs, out):
                 weigh_half(p - 2)
         last = BLOCKS - 1
         for i, bank in enumerate(last_banks):
-            turn_back(i // 2, terms_of[i], False)
+            if i < len(COPY_STEPS):
+                turn_back(i // 2, terms_of[i], False)
             turn_and_weigh(last, last_parts[i], bank)
         for u in (3, 5, 4):
             turn_back(u // 2, terms_of[u], u == 4)

import math

import concourse.mybir as mybir

BF16, F32, U16 = mybir.dt.bfloat16, mybir.dt.float32, mybir.dt.uint16
ALU = mybir.AluOpType
ACT = mybir.ActivationFunctionType
X_AXIS = mybir.AxisListType.X

C = 128
S = 512
K = 8
DH = 16
N = S * K
PIECE = 512
NODES = PIECE // K
PIECES = N // PIECE
HEADS = C // DH
BLOCK = 128
BLOCKS = S // BLOCK
PER_BLOCK = BLOCK // NODES
PER_BANK = 4
HELPED = (0, 1, 2, 3, 4)
BEHIND_RUN = 4
FIRST_STEP = 2
LAST_STEPS = (4, 2, 1, 1)
COPY_STEPS = (4, 3, 1)

FLOPS = 2 * C * (2 * C) * N + 2 * C * (2 * C) * S + 2 * C * C * N


def tile_attnno_kernel(tc, x, wkv, wqr, bqr, same_head, offs, out):
    nc = tc.nc
    with (
        tc.tile_pool(name="held", bufs=1) as held,
        tc.psum_pool(name="psum", bufs=1) as psum,
    ):
        offsets = held.tile([C, N // 16], U16, name="offsets")
        x_sb = held.tile([C, S], BF16, name="x_sb")
        wkv_sb = held.tile([C, 2 * C], BF16, name="wkv_sb")
        wqr_sb = held.tile([C, 2 * C], BF16, name="wqr_sb")
        biases = held.tile([C, 2], F32, name="biases")
        bias_q = biases[:, 0:1]
        bias_res = biases[:, 1:2]
        for half in (slice(0, S // 2), slice(S // 2, S)):
            nc.sync.dma_start(x_sb[:, half], x[:, half])
        nc.sync.dma_start(wqr_sb[:], wqr)
        nc.sync.dma_start(offsets[:], offs)
        nc.sync.dma_start(wkv_sb[:], wkv)
        nc.sync.dma_start(biases[:], bqr.rearrange("(a p) o -> p (a o)", p=C))

        identity = held.tile([BLOCK, BLOCK], F32, name="identity")
        distance = held.tile([BLOCK, BLOCK], F32, name="distance")
        nc.gpsimd.iota(distance[:], [[1, BLOCK]], base=0, channel_multiplier=-1, allow_small_or_imprecise_dtypes=True)
        nc.gpsimd.tensor_single_scalar(identity[:], distance[:], 0.0, ALU.is_equal)
        ends = distance[:].rearrange("e (g d) -> e g d", d=DH)
        signs = held.tile([C, HEADS], F32, name="signs")
        head_columns = held.tile([C, HEADS], BF16, name="head_columns")[:]
        nc.gpsimd.tensor_tensor(signs[:], ends[:, :, 0], ends[:, :, DH - 1], ALU.mult)
        nc.gpsimd.tensor_single_scalar(head_columns, signs[:], 0.0, ALU.is_le)

        banks = [psum.tile([C, PIECE], F32, name="bank%d" % i) for i in range(8)]
        query_banks = banks[6:8]
        key_banks = banks
        score_banks = key_banks[1:4]
        value_banks = [key_banks[0], key_banks[7], score_banks[0], score_banks[1]]
        value_banks += value_banks[1:4]
        turned_banks = [value_banks[0], key_banks[6], key_banks[5], score_banks[2]]
        turned_banks += turned_banks[0:4:2]
        value_banks.append(turned_banks[1])
        last_banks = [turned_banks[3], value_banks[6], key_banks[4], value_banks[7]]
        out_banks = [value_banks[5], value_banks[4]]

        h = held.tile([C, S], BF16, name="h")
        quarters = [slice(b * BLOCK, (b + 1) * BLOCK) for b in range(BLOCKS)]
        for columns in quarters:
            nc.scalar.activation(h[:, columns], x_sb[:, columns], ACT.Gelu)

        q = held.tile([C, S], F32, name="q")
        prod = held.tile([C, K, S], BF16, name="prod")
        val = held.tile([C, BLOCKS, K, BLOCK], F32, name="val")
        weighted = held.tile([BLOCK, BLOCKS, K, C], F32, name="weighted")
        result = held.tile([C, S], F32, name="result")

        def nodes_of(p):
            return slice(p * NODES, (p + 1) * NODES)

        def parts_of(steps):
            return [slice(sum(steps[:i]), sum(steps[: i + 1])) for i in range(len(steps))]

        halves = parts_of([PER_BANK, PER_BANK])
        last_parts = parts_of(LAST_STEPS)

        def gathered(bank, weight_columns, p):
            picked = h[:].indirect(offsets[:, p * (PIECE // 16) : (p + 1) * (PIECE // 16)])
            nc.tensor.matmul(bank[:], wkv_sb[:, weight_columns], picked, start=True, stop=True)
            return bank[:].rearrange("c (n t) -> c t n", t=K)

        def keys_of_piece(p):
            key = gathered(key_banks[p], slice(0, C), p)
            nc.vector.tensor_tensor(
                prod[:, :, nodes_of(p)], key, q[:, nodes_of(p)].unsqueeze(1).to_broadcast([C, K, NODES]), ALU.mult
            )

        def values_of_piece(p):
            value = gathered(value_banks[p], slice(C, 2 * C), p)
            b, k = divmod(p, PER_BLOCK)
            for part in parts_of(COPY_STEPS) if p == PIECES - 1 else halves if k else [slice(0, K)]:
                nc.scalar.copy(val[:, b, part, k * NODES : (k + 1) * NODES], value[:, part, :])

        groups = [range(0, 1), range(1, 2), range(2, BLOCKS)]

        def score_view(group):
            return score_banks[group][:, 0 : len(groups[group]) * K * HEADS].rearrange(
                "n (i t g) -> n i t g", t=K, g=HEADS
            )

        def scores(group):
            for i, b in enumerate(groups[group]):
                for t in range(K):
                    nc.tensor.matmul(
                        score_view(group)[:, i, t, :], prod[:, t, b * BLOCK : (b + 1) * BLOCK], head_columns,
                        start=True, stop=True,
                    )

        share = held.tile([BLOCK, BLOCKS, HEADS, K], F32, name="share")
        top = held.tile([BLOCK, BLOCKS, HEADS], F32, name="top")
        rden = held.tile([BLOCK, BLOCKS, HEADS], F32, name="rden")

        def blocks_of(group):
            return slice(groups[group].start, groups[group].stop)

        def over_neighbours(per_head, group):
            return per_head[:, blocks_of(group)].unsqueeze(3).to_broadcast([BLOCK, len(groups[group]), HEADS, K])

        def maxima(group):
            score = score_view(group).rearrange("n i t g -> n i g t")
            nc.vector.tensor_reduce(top[:, blocks_of(group)], score, X_AXIS, ALU.max)

        def exponentials(group):
            score = score_view(group).rearrange("n i t g -> n i g t")
            mine = share[:, blocks_of(group)]
            nc.vector.tensor_tensor(mine, score, over_neighbours(top, group), ALU.subtract)
            nc.scalar.activation(mine, mine, ACT.Exp, scale=1.0 / math.sqrt(DH))

        def denominators(group):
            nc.vector.tensor_reduce(rden[:, blocks_of(group)], share[:, blocks_of(group)], X_AXIS, ALU.add)

        def reciprocals(group):
            nc.vector.reciprocal(rden[:, blocks_of(group)], rden[:, blocks_of(group)])

        def normalise(group):
            mine = share[:, blocks_of(group)]
            nc.vector.tensor_tensor(mine, mine, over_neighbours(rden, group), ALU.mult)

        def turn_and_weigh(b, part, bank):
            count = part.stop - part.start
            turned = bank[:, 0 : count * C].rearrange("n (t c) -> n t c", c=C)
            for t in range(count):
                nc.tensor.transpose(turned[:, t, :], val[:, b, part.start + t, :], identity[:])
            nc.vector.tensor_tensor(
                weighted[:, b, part].rearrange("n t (g d) -> n t g d", d=DH),
                turned.rearrange("n t (g d) -> n t g d", d=DH),
                share[:, b, :, part].rearrange("n g t -> n t g").unsqueeze(3).to_broadcast([BLOCK, count, HEADS, DH]),
                ALU.mult,
            )

        def halved(u):
            b, first = u // 2, (u % 2) * PER_BANK
            two = held.tile([BLOCK, 2, C], F32, name="two%d" % u)
            nc.gpsimd.tensor_tensor(two[:], weighted[:, b, first : first + 2], weighted[:, b, first + 2 : first + 4], ALU.add)
            return two

        out_columns = [slice(0, S - BLOCK), slice(S - BLOCK, S)]

        def turn_back(b, terms, closes):
            bank = out_banks[b // (BLOCKS - 1)]
            count = terms.shape[1]
            for t in range(count):
                nc.tensor.matmul(
                    bank[:, b * BLOCK : (b + 1) * BLOCK], terms[:, t, :], identity[:],
                    start=False, stop=(closes and t == count - 1), is_transpose=True,
                )

        def linear_branch(i):
            columns = out_columns[i]
            nc.tensor.matmul(out_banks[i][:, columns], wqr_sb[:, C : 2 * C], h[:, columns], start=True, stop=False)

        for b, columns in enumerate(quarters):
            nc.tensor.matmul(query_banks[b // 2][:, columns], wqr_sb[:, 0:C], h[:, columns], start=True, stop=True)
        for bank, half in zip(query_banks, (slice(0, S // 2), slice(S // 2, S))):
            nc.scalar.activation(q[:, half], bank[:, half], ACT.Identity, bias=bias_q)
        exp_table = held.tile([C, 1], F32, name="exp_table")
        nc.scalar.activation(exp_table[:], q[:, S - 1 : S], ACT.Exp, scale=0.0)

        for p in range(PIECES):
            keys_of_piece(p)
        values_of_piece(0)
        scores(0)
        scores(1)
        scores(2)
        for stage in (maxima, exponentials, denominators, reciprocals, normalise):
            for group in range(len(groups)):
                stage(group)

        terms_of = []

        def weigh_half(u):
            b, k = divmod(u, PER_BLOCK)
            part = slice(k * PER_BANK, (k + 1) * PER_BANK)
            if u == BEHIND_RUN:
                turn_and_weigh(b, slice(part.start, part.start + FIRST_STEP), last_banks[2])
                turn_and_weigh(b, slice(part.start + FIRST_STEP, part.stop), turned_banks[u])
            else:
                turn_and_weigh(b, part, turned_banks[u])
            terms_of.append(halved(u)[:] if u in HELPED else weighted[:, b, part])

        for p in range(1, PIECES):
            values_of_piece(p)
            if p == PIECES - 1:
                linear_branch(0)
                linear_branch(1)
            if p >= 3 and p % 2:
                weigh_half(p - 3)
                weigh_half(p - 2)
        last = BLOCKS - 1
        for i, bank in enumerate(last_banks):
            if i < len(COPY_STEPS):
                turn_back(i // 2, terms_of[i], False)
            turn_and_weigh(last, last_parts[i], bank)
        for u in (3, 5, 4):
            turn_back(u // 2, terms_of[u], u == 4)
        turn_back(last, weighted[:, last], True)

        for bank, columns in zip(out_banks, out_columns):
            nc.scalar.activation(result[:, columns], bank[:, columns], ACT.Gelu, bias=bias_res)
            nc.sync.dma_start(out[:, columns], result[:, columns])
